import numpy as np
import ml_dtypes


def mxq(x, axis, fmt="e4m3"):
    dtype, down = {"e4m3": (ml_dtypes.float8_e4m3fn, 7), "e5m2": (ml_dtypes.float8_e5m2, 14)}[fmt]
    v = np.moveaxis(np.asarray(x, np.float32).astype(ml_dtypes.bfloat16).astype(np.float64), axis, -1)
    blocks = v.reshape(v.shape[:-1] + (-1, 32))
    amax = np.abs(blocks).max(-1, keepdims=True)
    byte = np.maximum(np.where(amax > 0, np.frexp(amax)[1] - 1 + 127, 0) - down, 1)
    scale = np.exp2(byte - 127.0)
    codes = (blocks / scale).astype(np.float32).astype(dtype).astype(np.float64)
    return np.moveaxis((codes * scale).reshape(v.shape), -1, axis)


WIDE = False


def mx_kscale(k):
    if not WIDE:
        return np.ones(k)
    levels = np.array([10, -10, 5, -5, 0])
    a = np.random.permutation(np.resize(levels, k // 512 * 4)).reshape(k // 512, 4)
    idx = np.arange(k)
    return np.exp2(a[idx // 512, idx % 128 // 32])


BF16 = ml_dtypes.bfloat16


def bf(x):
    return np.asarray(x, np.float32).astype(BF16)


def f64(x):
    return np.asarray(x).astype(np.float64)


B, S, D, P, PW, L = 2, 128, 512, 32, 2, 2
K = P * D
EPS = 1e-5


def layer_norm(v, g, b):
    m = v.mean(-1, keepdims=True)
    var = np.square(v - m).mean(-1, keepdims=True)
    return (v - m) * (1.0 / np.sqrt(var + EPS)) * g + b


def setup_inputs():
    n = np.random.standard_normal
    s = mx_kscale(K)
    return {"e": bf(n((B, S, K)) * 0.8 * s),
            "h": bf(n((B, S, D)) * 0.8 + 0.3),
            "ent_pw": bf(n((K, D)) / np.sqrt(K) / s[:, None]),
            "ent_pb": bf(n(D) * 0.2),
            "ln3_g": bf(1.0 + 0.1 * n(D)),
            "ln3_b": bf(0.2 * n(D) + 0.2),
            "path_w": bf(n((PW, D, D)) * 0.7 / np.sqrt(D)),
            "path_b": bf(n((PW, D)) * 0.2),
            "phase": bf(n((PW, D))),
            "ln4_g": bf(1.0 + 0.1 * n(D)),
            "ln4_b": bf(0.2 * n(D))}


def reference(e, h, ent_pw, ent_pb, ln3_g, ln3_b, path_w, path_b, phase, ln4_g, ln4_b):
    ent = (mxq(f64(e), 2, "e4m3") @ mxq(f64(ent_pw), 0, "e4m3")) + f64(ent_pb)
    hn = layer_norm(f64(h) + ent, f64(ln3_g), f64(ln3_b))
    t = (mxq(hn, 2, "e4m3")[None] @ mxq(f64(path_w), 1, "e4m3")[:, None]) + f64(path_b)[:, None, None, :]
    mod = np.cos(f64(phase)) + np.sin(f64(phase))
    interf = np.sum(t * mod[:, None, None, :], axis=0)
    return layer_norm(hn + interf, f64(ln4_g), f64(ln4_b))

@@ -1,0 +1,400 @@
+from contextlib import ExitStack
+
+import concourse.masks as masks
+import concourse.mybir as mybir
+
+F32 = mybir.dt.float32
+BF16 = mybir.dt.bfloat16
+U32 = mybir.dt.uint32
+U8 = mybir.dt.uint8
+FP8X4 = mybir.dt.float8_e4m3fn_x4
+ALU = mybir.AluOpType
+ACT = mybir.ActivationFunctionType
+
+P = 128
+PACK = 4
+K_PASS = P * PACK
+TILES = 2
+D = 512
+K = 16384
+SLICES = D // P
+EPS = 1e-5
+
+STEP_PASSES = 2
+STEPS = K // (STEP_PASSES * K_PASS)
+E_LOAD_STEPS = 2
+E_LOADS = STEPS // E_LOAD_STEPS
+W_AHEAD = 3
+E_AHEAD = 2
+
+V_COLS = 288
+
+FLOPS = 2 * TILES * P * K * D + 2 * 2 * TILES * P * D * D
+
+ENT_PB, LN3_G, LN3_B, PATH_B, PHASE, LN4_G, LN4_B = 0, 1, 2, 3, 5, 7, 8
+LOADED = 9
+MOD = 9
+SHIFT = 11
+COLUMNS = 12
+
+TWO_PI_HI = 6.28125
+TWO_PI_MID = 0.0019353071693331003
+TWO_PI_LO = 1.0253131677018246e-11
+INV_TWO_PI = 0.15915493667125702
+PI_BELOW = 3.141592502593994
+ROUND_MAGIC = 12582912.0
+
+
+def tile_quantuminspiredneuralcore_pb_k_kernel(
+    tc, e, h, ent_pw, ent_pb, ln3_g, ln3_b, path_w, path_b, phase, ln4_g, ln4_b, out
+):
+    nc = tc.nc
+    with ExitStack() as ctx:
+        consts = ctx.enter_context(tc.tile_pool(name="consts", bufs=1))
+        e_raws = ctx.enter_context(tc.tile_pool(name="e_raws", bufs=E_AHEAD + 1))
+        w_raws = ctx.enter_context(tc.tile_pool(name="w_raws", bufs=W_AHEAD + 1))
+        grouped = ctx.enter_context(tc.tile_pool(name="grouped", bufs=3))
+        w_quant = ctx.enter_context(tc.tile_pool(name="w_quant", bufs=3))
+        e_quant = ctx.enter_context(tc.tile_pool(name="e_quant", bufs=4))
+        work = ctx.enter_context(tc.tile_pool(name="work", bufs=1))
+        small = ctx.enter_context(tc.tile_pool(name="small", bufs=1))
+        accs = ctx.enter_context(tc.psum_pool(name="accs", bufs=1))
+        banks = ctx.enter_context(tc.psum_pool(name="banks", bufs=6))
+
+        def load_weight_rows(view):
+            w_raw = w_raws.tile([P, STEP_PASSES, PACK, D], BF16, name="w_raw", tag="w_raw")
+            nc.sync.dma_start(out=w_raw[:], in_=view)
+            return w_raw
+
+        def load_w(step):
+            rows = ent_pw[step * STEP_PASSES * K_PASS : (step + 1) * STEP_PASSES * K_PASS, :]
+            return load_weight_rows(rows.rearrange("(c p t) n -> p c t n", p=P, t=PACK))
+
+        def load_e(load):
+            width = E_LOAD_STEPS * STEP_PASSES * K_PASS
+            e_raw = e_raws.tile([P, TILES, width], BF16, name="e_raw", tag="e_raw")
+            nc.sync.dma_start(
+                out=e_raw[:],
+                in_=e[:, :, load * width : (load + 1) * width].rearrange("b s k -> s b k"),
+            )
+            return e_raw
+
+        def regroup_weights(w_raw):
+            w_grp = grouped.tile(
+                [P, STEP_PASSES, D, PACK], BF16, name="w_grp", tag="w_grp", align_bytes=64
+            )
+            for c in range(STEP_PASSES):
+                nc.vector.tensor_copy(
+                    out=w_grp[:, c, 0:V_COLS, :].rearrange("p (a i) t -> p a t i", i=4),
+                    in_=w_raw[:, c, :, 0:V_COLS].rearrange("p t (a i) -> p a t i", i=4),
+                )
+                nc.scalar.copy(
+                    out=w_grp[:, c, V_COLS:D, :].rearrange("p (a i) t -> p a t i", i=4),
+                    in_=w_raw[:, c, :, V_COLS:D].rearrange("p t (a i) -> p a t i", i=4),
+                )
+            return w_grp
+
+        def quantise_weights(w_grp, pool):
+            codes = pool.tile([P, STEP_PASSES * D], U32, name="w_codes", tag="w_codes", align_bytes=64)
+            scales = pool.tile([P, STEP_PASSES * D], U8, name="w_scales", tag="w_scales", align_bytes=64)
+            nc.vector.quantize_mx(
+                out=codes[:].bitcast(FP8X4),
+                scales=scales[:],
+                in_=w_grp[:].rearrange("p c n t -> p (c n t)"),
+            )
+            return codes, scales
+
+        def transpose_e(e_raw, half):
+            words = K_PASS // 2
+            planes = []
+            for i in range(TILES):
+                e_words = e_raw[:, i, :].bitcast(F32)
+                bank = banks.tile([P, STEP_PASSES, 2, P], F32, name="e_bank", tag="bank")
+                for c in range(STEP_PASSES):
+                    first = (half * STEP_PASSES + c) * words
+                    for u in range(2):
+                        nc.tensor.transpose(
+                            out=bank[:, c, u, :],
+                            in_=e_words[:, first + u : first + words : 2],
+                            identity=ident_f32[:],
+                        )
+                planes.append(bank)
+            return planes
+
+        def copy_e(planes):
+            e_grp = grouped.tile(
+                [P, TILES * STEP_PASSES * P * 2], F32, name="e_grp", tag="e_grp", align_bytes=64
+            )
+            per_tile = STEP_PASSES * P * 2
+            for i in range(TILES):
+                nc.scalar.copy(
+                    out=e_grp[:, i * per_tile : (i + 1) * per_tile].rearrange(
+                        "p (c r u) -> p c r u", c=STEP_PASSES, u=2
+                    ),
+                    in_=planes[i][:].rearrange("p c u r -> p c r u"),
+                )
+            return e_grp
+
+        def quantise_e(e_grp):
+            codes = e_quant.tile([P, TILES * STEP_PASSES * P], U32, name="e_codes", tag="e_codes", align_bytes=64)
+            scales = e_quant.tile([P, TILES * STEP_PASSES * P], U8, name="e_scales", tag="e_scales", align_bytes=64)
+            nc.vector.quantize_mx(
+                out=codes[:].bitcast(FP8X4), scales=scales[:], in_=e_grp[:].bitcast(BF16)
+            )
+            return codes, scales
+
+        def multiply(step, e_op, w_op):
+            e_codes, e_scales = e_op
+            w_codes, w_scales = w_op
+            for c in range(STEP_PASSES):
+                k_pass = step * STEP_PASSES + c
+                w_cols = slice(c * D, (c + 1) * D)
+                for i in range(TILES):
+                    e_cols = slice((i * STEP_PASSES + c) * P, (i * STEP_PASSES + c + 1) * P)
+                    nc.tensor.matmul_mx(
+                        out=acc[i][:],
+                        lhsT=e_codes[:, e_cols].bitcast(FP8X4),
+                        lhsT_scale=e_scales[:, e_cols],
+                        rhs=w_codes[:, w_cols].bitcast(FP8X4),
+                        rhs_scale=w_scales[:, w_cols],
+                        start=(k_pass == 0),
+                        stop=(k_pass == K // K_PASS - 1),
+                    )
+
+        vec_rows = consts.tile([P, D], BF16, name="vec_rows")
+        nc.vector.memset(vec_rows[:], 0.0)
+        for row, vector in (
+            (ENT_PB, ent_pb),
+            (LN3_G, ln3_g),
+            (LN3_B, ln3_b),
+            (LN4_G, ln4_g),
+            (LN4_B, ln4_b),
+        ):
+            nc.scalar.dma_start(
+                out=vec_rows[row : row + 1, :], in_=vector.rearrange("(o d) -> o d", o=1)
+            )
+        nc.scalar.dma_start(out=vec_rows[PATH_B : PATH_B + 2, :], in_=path_b)
+        nc.scalar.dma_start(out=vec_rows[PHASE : PHASE + 2, :], in_=phase)
+        h_sb = consts.tile([P, TILES, D], BF16, name="h_sb")
+        nc.scalar.dma_start(out=h_sb[:], in_=h.rearrange("b s d -> s b d"))
+
+        path_raw = load_weight_rows(path_w.rearrange("w (t p) n -> p w t n", p=P))
+        e_raw_of = {}
+        w_raw_of = {}
+        for load in range(E_AHEAD):
+            e_raw_of[load] = load_e(load)
+        for step in range(W_AHEAD):
+            w_raw_of[step] = load_w(step)
+
+        ident_f32 = consts.tile([P, P], F32, name="ident_f32")
+        masks.make_identity(nc, ident_f32[:])
+        ident_bf16 = consts.tile([P, P], BF16, name="ident_bf16")
+        masks.make_identity(nc, ident_bf16[:])
+        eps = consts.tile([P, 1], F32, name="eps")
+        nc.vector.memset(eps[:], EPS)
+
+        vec_bank = banks.tile([P, SLICES, P], BF16, name="vec_bank", tag="bank")
+        for s in range(SLICES):
+            nc.tensor.transpose(
+                out=vec_bank[:, s, :], in_=vec_rows[:, s * P : (s + 1) * P], identity=ident_bf16[:]
+            )
+        cols = consts.tile([P, SLICES, COLUMNS], F32, name="cols")
+        nc.vector.tensor_copy(out=cols[:, :, 0:LOADED], in_=vec_bank[:, :, 0:LOADED])
+
+        phases = cols[:, :, PHASE : PHASE + 2]
+        turns = consts.tile([P, SLICES, 2], F32, name="turns")
+        nc.vector.tensor_scalar(
+            out=turns[:], in0=phases, scalar1=INV_TWO_PI, scalar2=ROUND_MAGIC, op0=ALU.mult, op1=ALU.add
+        )
+        nc.vector.tensor_scalar(
+            out=turns[:], in0=turns[:], scalar1=ROUND_MAGIC, scalar2=None, op0=ALU.subtract
+        )
+        angle = consts.tile([P, SLICES, 2], F32, name="angle")
+        nc.vector.scalar_tensor_tensor(
+            out=angle[:], in0=turns[:], scalar=-TWO_PI_HI, in1=phases, op0=ALU.mult, op1=ALU.add
+        )
+        for piece in (TWO_PI_MID, TWO_PI_LO):
+            nc.vector.scalar_tensor_tensor(
+                out=angle[:], in0=turns[:], scalar=-piece, in1=angle[:], op0=ALU.mult, op1=ALU.add
+            )
+        nc.vector.tensor_scalar(
+            out=angle[:], in0=angle[:], scalar1=PI_BELOW, scalar2=-PI_BELOW, op0=ALU.min, op1=ALU.max
+        )
+        sin_full = consts.tile([P, SLICES, 2], F32, name="sin_full")
+        nc.scalar.activation(out=sin_full[:], in_=angle[:], func=ACT.Sin)
+        sin_half = consts.tile([P, SLICES, 2], F32, name="sin_half")
+        nc.scalar.activation(out=sin_half[:], in_=angle[:], func=ACT.Sin, scale=0.5)
+        half_sq = consts.tile([P, SLICES, 2], F32, name="half_sq")
+        nc.vector.tensor_tensor(out=half_sq[:], in0=sin_half[:], in1=sin_half[:], op=ALU.mult)
+        table_warm = consts.tile([P, 1], F32, name="table_warm")
+        nc.scalar.activation(
+            out=table_warm[:], in_=half_sq[:, 0, 0:1], func=ACT.Sqrt, bias=eps[:, 0:1]
+        )
+        sin_less = consts.tile([P, SLICES, 2], F32, name="sin_less")
+        nc.vector.scalar_tensor_tensor(
+            out=sin_less[:], in0=half_sq[:], scalar=-2.0, in1=sin_full[:], op0=ALU.mult, op1=ALU.add
+        )
+        nc.vector.tensor_scalar(
+            out=cols[:, :, MOD : MOD + 2], in0=sin_less[:], scalar1=1.0, scalar2=None, op0=ALU.add
+        )
+        weighted_b = consts.tile([P, SLICES, 2], F32, name="weighted_b")
+        nc.vector.tensor_tensor(
+            out=weighted_b[:], in0=cols[:, :, PATH_B : PATH_B + 2], in1=cols[:, :, MOD : MOD + 2], op=ALU.mult
+        )
+        nc.vector.tensor_tensor(
+            out=cols[:, :, SHIFT : SHIFT + 1], in0=weighted_b[:, :, 0:1], in1=weighted_b[:, :, 1:2], op=ALU.add
+        )
+        nc.vector.tensor_tensor(
+            out=cols[:, :, SHIFT : SHIFT + 1],
+            in0=cols[:, :, SHIFT : SHIFT + 1],
+            in1=cols[:, :, LN3_B : LN3_B + 1],
+            op=ALU.add,
+        )
+
+        def spread(column, name):
+            bank = banks.tile([P, D], F32, name=name, tag="bank")
+            for s in range(SLICES):
+                nc.tensor.transpose(
+                    out=bank[:, s * P : (s + 1) * P],
+                    in_=cols[:, s, column : column + 1].to_broadcast([P, P]),
+                    identity=ident_f32[:],
+                )
+            return bank
+
+        def spread_to_sbuf(column, name):
+            row = consts.tile([P, D], F32, name=name)
+            nc.scalar.copy(out=row[:], in_=spread(column, name + "_bank")[:])
+            return row
+
+        bias_bank = spread(ENT_PB, "bias_bank")
+        h_bias = consts.tile([P, TILES, D], F32, name="h_bias")
+        for i in range(TILES):
+            nc.vector.tensor_tensor(out=h_bias[:, i, :], in0=bias_bank[:], in1=h_sb[:, i, :], op=ALU.add)
+        ln3_g_row = spread_to_sbuf(LN3_G, "ln3_g_row")
+        ln3_b_row = spread_to_sbuf(LN3_B, "ln3_b_row")
+        shift_row = spread_to_sbuf(SHIFT, "shift_row")
+        mod_row = [spread_to_sbuf(MOD + w, "mod_row%d" % w) for w in range(2)]
+        ln4_g_row = spread_to_sbuf(LN4_G, "ln4_g_row")
+        ln4_b_row = spread_to_sbuf(LN4_B, "ln4_b_row")
+
+        path_op = quantise_weights(regroup_weights(path_raw), consts)
+
+        acc = [accs.tile([P, D], F32, name="acc%d" % i) for i in range(TILES)]
+
+        def planes_of(step):
+            return transpose_e(e_raw_of[step // E_LOAD_STEPS], step % E_LOAD_STEPS)
+
+        e_planes = {0: planes_of(0)}
+        e_op = {0: quantise_e(copy_e(e_planes[0]))}
+        e_planes[1] = planes_of(1)
+        w_grp_of = {}
+        for t in range(STEPS + 1):
+            if t % E_LOAD_STEPS == 0 and t // E_LOAD_STEPS + E_AHEAD < E_LOADS:
+                e_raw_of[t // E_LOAD_STEPS + E_AHEAD] = load_e(t // E_LOAD_STEPS + E_AHEAD)
+            if t + W_AHEAD < STEPS:
+                w_raw_of[t + W_AHEAD] = load_w(t + W_AHEAD)
+            if t + 2 < STEPS:
+                e_planes[t + 2] = planes_of(t + 2)
+            if t >= 1:
+                w_op = quantise_weights(w_grp_of[t - 1], w_quant)
+            if t + 1 < STEPS:
+                e_grp = copy_e(e_planes[t + 1])
+            if t < STEPS:
+                w_grp_of[t] = regroup_weights(w_raw_of[t])
+            if t + 1 < STEPS:
+                e_op[t + 1] = quantise_e(e_grp)
+            if t >= 1:
+                multiply(t - 1, e_op[t - 1], w_op)
+
+        def centre_and_scale(x, x_sum, gain_row, label):
+            neg_mean = small.tile([P, 1], F32, name="neg_mean" + label)
+            nc.vector.tensor_scalar(
+                out=neg_mean[:], in0=x_sum[:], scalar1=-1.0 / D, scalar2=None, op0=ALU.mult
+            )
+            squares = work.tile([P, D], F32, name="squares" + label)
+            sum_sq = small.tile([P, 1], F32, name="sum_sq" + label)
+            nc.scalar.activation(
+                out=squares[:], in_=x[:], func=ACT.Square, bias=neg_mean[:, 0:1], accum_out=sum_sq[:]
+            )
+            centred = work.tile([P, D], F32, name="centred" + label)
+            nc.vector.scalar_tensor_tensor(
+                out=centred[:], in0=x[:], scalar=neg_mean[:, 0:1], in1=gain_row[:], op0=ALU.add, op1=ALU.mult
+            )
+            std = small.tile([P, 1], F32, name="std" + label)
+            nc.scalar.activation(
+                out=std[:], in_=sum_sq[:], func=ACT.Sqrt, bias=eps[:, 0:1], scale=1.0 / D
+            )
+            rstd = small.tile([P, 1], F32, name="rstd" + label)
+            nc.vector.reciprocal(out=rstd[:], in_=std[:])
+            return centred, rstd
+
+        def scale_and_shift(centred, rstd, shift, name):
+            result = work.tile([P, D], F32, name=name)
+            nc.vector.scalar_tensor_tensor(
+                out=result[:], in0=centred[:], scalar=rstd[:, 0:1], in1=shift[:], op0=ALU.mult, op1=ALU.add
+            )
+            return result
+
+        def first_norm(i):
+            x = work.tile([P, D], F32, name="x%d" % i)
+            x_sum = small.tile([P, 1], F32, name="x_sum%d" % i)
+            nc.vector.scalar_tensor_tensor(
+                out=x[:], in0=acc[i][:], scalar=1.0, in1=h_bias[:, i, :], op0=ALU.mult, op1=ALU.add,
+                accum_out=x_sum[:],
+            )
+            centred, rstd = centre_and_scale(x, x_sum, ln3_g_row, "_a%d" % i)
+            hn = scale_and_shift(centred, rstd, ln3_b_row, "hn%d" % i)
+            hn_shifted = scale_and_shift(centred, rstd, shift_row, "hn_shifted%d" % i)
+            return hn, hn_shifted
+
+        def pathways(i, hn):
+            hn_bank = banks.tile([P, PACK, P], F32, name="hn_bank", tag="bank")
+            for t in range(PACK):
+                nc.tensor.transpose(
+                    out=hn_bank[:, t, :], in_=hn[:, t * P : (t + 1) * P], identity=ident_f32[:]
+                )
+            hn_grp = work.tile([P, P, PACK], BF16, name="hn_grp%d" % i, align_bytes=64)
+            nc.scalar.copy(out=hn_grp[:], in_=hn_bank[:].rearrange("p t r -> p r t"))
+            hn_codes = work.tile([P, P], U32, name="hn_codes%d" % i, align_bytes=64)
+            hn_scales = work.tile([P, P], U8, name="hn_scales%d" % i, align_bytes=64)
+            nc.vector.quantize_mx(
+                out=hn_codes[:].bitcast(FP8X4),
+                scales=hn_scales[:],
+                in_=hn_grp[:].rearrange("p r t -> p (r t)"),
+            )
+            path_codes, path_scales = path_op
+            products = []
+            for w in range(2):
+                product = banks.tile([P, D], F32, name="product", tag="bank")
+                nc.tensor.matmul_mx(
+                    out=product[:],
+                    lhsT=hn_codes[:].bitcast(FP8X4),
+                    lhsT_scale=hn_scales[:],
+                    rhs=path_codes[:, w * D : (w + 1) * D].bitcast(FP8X4),
+                    rhs_scale=path_scales[:, w * D : (w + 1) * D],
+                    start=True,
+                    stop=True,
+                )
+                products.append(product)
+            return products
+
+        def second_norm(i, hn_shifted, products):
+            first = work.tile([P, D], F32, name="first%d" % i)
+            nc.vector.tensor_tensor(out=first[:], in0=products[0][:], in1=mod_row[0][:], op=ALU.mult)
+            second = work.tile([P, D], F32, name="second%d" % i)
+            nc.vector.tensor_tensor(out=second[:], in0=products[1][:], in1=mod_row[1][:], op=ALU.mult)
+            nc.vector.tensor_tensor(out=first[:], in0=first[:], in1=hn_shifted[:], op=ALU.add)
+            y = work.tile([P, D], F32, name="y%d" % i)
+            y_sum = small.tile([P, 1], F32, name="y_sum%d" % i)
+            nc.vector.scalar_tensor_tensor(
+                out=y[:], in0=first[:], scalar=1.0, in1=second[:], op0=ALU.mult, op1=ALU.add,
+                accum_out=y_sum[:],
+            )
+            centred, rstd = centre_and_scale(y, y_sum, ln4_g_row, "_b%d" % i)
+            result = scale_and_shift(centred, rstd, ln4_b_row, "result%d" % i)
+            nc.sync.dma_start(out=out[i], in_=result[:])
+
+        normed = [first_norm(i) for i in range(TILES)]
+        products = [pathways(i, normed[i][0]) for i in range(TILES)]
+        for i in range(TILES):
+            second_norm(i, normed[i][1], products[i])

@@ -24,7 +24,7 @@ STEP_PASSES = 2
 STEPS = K // (STEP_PASSES * K_PASS)
 E_LOAD_STEPS = 2
 E_LOADS = STEPS // E_LOAD_STEPS
-W_AHEAD = 3
+W_AHEAD = 4
 E_AHEAD = 2
 
 V_COLS = 288
@@ -83,11 +83,11 @@ def tile_quantuminspiredneuralcore_pb_k_kernel(
             w_grp = grouped.tile(
                 [P, STEP_PASSES, D, PACK], BF16, name="w_grp", tag="w_grp", align_bytes=64
             )
+            nc.vector.tensor_copy(
+                out=w_grp[:, :, 0:V_COLS, :].rearrange("p c (a i) t -> p c a t i", i=4),
+                in_=w_raw[:, :, :, 0:V_COLS].rearrange("p c t (a i) -> p c a t i", i=4),
+            )
             for c in range(STEP_PASSES):
-                nc.vector.tensor_copy(
-                    out=w_grp[:, c, 0:V_COLS, :].rearrange("p (a i) t -> p a t i", i=4),
-                    in_=w_raw[:, c, :, 0:V_COLS].rearrange("p t (a i) -> p a t i", i=4),
-                )
                 nc.scalar.copy(
                     out=w_grp[:, c, V_COLS:D, :].rearrange("p (a i) t -> p a t i", i=4),
                     in_=w_raw[:, c, :, V_COLS:D].rearrange("p t (a i) -> p a t i", i=4),
@@ -161,37 +161,38 @@ def tile_quantuminspiredneuralcore_pb_k_kernel(
                         stop=(k_pass == K // K_PASS - 1),
                     )
 
+        ctx.enter_context(tc.manual_schedule())
+
         vec_rows = consts.tile([P, D], BF16, name="vec_rows")
         nc.vector.memset(vec_rows[:], 0.0)
         for row, vector in (
-            (ENT_PB, ent_pb),
-            (LN3_G, ln3_g),
-            (LN3_B, ln3_b),
-            (LN4_G, ln4_g),
-            (LN4_B, ln4_b),
+            (PHASE, phase),
+            (PATH_B, path_b),
+            (ENT_PB, ent_pb.rearrange("(o d) -> o d", o=1)),
+            (LN3_G, ln3_g.rearrange("(o d) -> o d", o=1)),
+            (LN3_B, ln3_b.rearrange("(o d) -> o d", o=1)),
+            (LN4_G, ln4_g.rearrange("(o d) -> o d", o=1)),
+            (LN4_B, ln4_b.rearrange("(o d) -> o d", o=1)),
         ):
-            nc.scalar.dma_start(
-                out=vec_rows[row : row + 1, :], in_=vector.rearrange("(o d) -> o d", o=1)
-            )
-        nc.scalar.dma_start(out=vec_rows[PATH_B : PATH_B + 2, :], in_=path_b)
-        nc.scalar.dma_start(out=vec_rows[PHASE : PHASE + 2, :], in_=phase)
+            nc.sync.dma_start(out=vec_rows[row : row + vector.shape[0], :], in_=vector)
         h_sb = consts.tile([P, TILES, D], BF16, name="h_sb")
         nc.scalar.dma_start(out=h_sb[:], in_=h.rearrange("b s d -> s b d"))
 
         path_raw = load_weight_rows(path_w.rearrange("w (t p) n -> p w t n", p=P))
-        e_raw_of = {}
-        w_raw_of = {}
-        for load in range(E_AHEAD):
-            e_raw_of[load] = load_e(load)
-        for step in range(W_AHEAD):
+        e_raw_of = {0: load_e(0)}
+        w_raw_of = {0: load_w(0)}
+        e_raw_of[1] = load_e(1)
+        for step in range(1, W_AHEAD):
             w_raw_of[step] = load_w(step)
 
-        ident_f32 = consts.tile([P, P], F32, name="ident_f32")
-        masks.make_identity(nc, ident_f32[:])
         ident_bf16 = consts.tile([P, P], BF16, name="ident_bf16")
         masks.make_identity(nc, ident_bf16[:])
+        ident_f32 = consts.tile([P, P], F32, name="ident_f32")
+        masks.make_identity(nc, ident_f32[:])
         eps = consts.tile([P, 1], F32, name="eps")
         nc.vector.memset(eps[:], EPS)
+        table_warm = consts.tile([P, 1], F32, name="table_warm")
+        nc.scalar.activation(out=table_warm[:], in_=eps[:], func=ACT.Sin)
 
         vec_bank = banks.tile([P, SLICES, P], BF16, name="vec_bank", tag="bank")
         for s in range(SLICES):
@@ -200,6 +201,23 @@ def tile_quantuminspiredneuralcore_pb_k_kernel(
             )
         cols = consts.tile([P, SLICES, COLUMNS], F32, name="cols")
         nc.vector.tensor_copy(out=cols[:, :, 0:LOADED], in_=vec_bank[:, :, 0:LOADED])
+
+        def spread(column, name):
+            bank = banks.tile([P, D], F32, name=name, tag="bank")
+            for s in range(SLICES):
+                nc.tensor.transpose(
+                    out=bank[:, s * P : (s + 1) * P],
+                    in_=cols[:, s, column : column + 1].to_broadcast([P, P]),
+                    identity=ident_f32[:],
+                )
+            return bank
+
+        def to_sbuf(bank, name):
+            row = consts.tile([P, D], F32, name=name)
+            nc.scalar.copy(out=row[:], in_=bank[:])
+            return row
+
+        bias_bank = spread(ENT_PB, "bias_bank")
 
         phases = cols[:, :, PHASE : PHASE + 2]
         turns = consts.tile([P, SLICES, 2], F32, name="turns")
@@ -224,12 +242,11 @@ def tile_quantuminspiredneuralcore_pb_k_kernel(
         nc.scalar.activation(out=sin_full[:], in_=angle[:], func=ACT.Sin)
         sin_half = consts.tile([P, SLICES, 2], F32, name="sin_half")
         nc.scalar.activation(out=sin_half[:], in_=angle[:], func=ACT.Sin, scale=0.5)
+
+        path_grp = regroup_weights(path_raw)
+
         half_sq = consts.tile([P, SLICES, 2], F32, name="half_sq")
         nc.vector.tensor_tensor(out=half_sq[:], in0=sin_half[:], in1=sin_half[:], op=ALU.mult)
-        table_warm = consts.tile([P, 1], F32, name="table_warm")
-        nc.scalar.activation(
-            out=table_warm[:], in_=half_sq[:, 0, 0:1], func=ACT.Sqrt, bias=eps[:, 0:1]
-        )
         sin_less = consts.tile([P, SLICES, 2], F32, name="sin_less")
         nc.vector.scalar_tensor_tensor(
             out=sin_less[:], in0=half_sq[:], scalar=-2.0, in1=sin_full[:], op0=ALU.mult, op1=ALU.add
@@ -244,40 +261,11 @@ def tile_quantuminspiredneuralcore_pb_k_kernel(
         nc.vector.tensor_tensor(
             out=cols[:, :, SHIFT : SHIFT + 1], in0=weighted_b[:, :, 0:1], in1=weighted_b[:, :, 1:2], op=ALU.add
         )
-        nc.vector.tensor_tensor(
-            out=cols[:, :, SHIFT : SHIFT + 1],
-            in0=cols[:, :, SHIFT : SHIFT + 1],
-            in1=cols[:, :, LN3_B : LN3_B + 1],
-            op=ALU.add,
-        )
-
-        def spread(column, name):
-            bank = banks.tile([P, D], F32, name=name, tag="bank")
-            for s in range(SLICES):
-                nc.tensor.transpose(
-                    out=bank[:, s * P : (s + 1) * P],
-                    in_=cols[:, s, column : column + 1].to_broadcast([P, P]),
-                    identity=ident_f32[:],
-                )
-            return bank
-
-        def spread_to_sbuf(column, name):
-            row = consts.tile([P, D], F32, name=name)
-            nc.scalar.copy(out=row[:], in_=spread(column, name + "_bank")[:])
-            return row
-
-        bias_bank = spread(ENT_PB, "bias_bank")
         h_bias = consts.tile([P, TILES, D], F32, name="h_bias")
         for i in range(TILES):
             nc.vector.tensor_tensor(out=h_bias[:, i, :], in0=bias_bank[:], in1=h_sb[:, i, :], op=ALU.add)
-        ln3_g_row = spread_to_sbuf(LN3_G, "ln3_g_row")
-        ln3_b_row = spread_to_sbuf(LN3_B, "ln3_b_row")
-        shift_row = spread_to_sbuf(SHIFT, "shift_row")
-        mod_row = [spread_to_sbuf(MOD + w, "mod_row%d" % w) for w in range(2)]
-        ln4_g_row = spread_to_sbuf(LN4_G, "ln4_g_row")
-        ln4_b_row = spread_to_sbuf(LN4_B, "ln4_b_row")
 
-        path_op = quantise_weights(regroup_weights(path_raw), consts)
+        path_op = quantise_weights(path_grp, consts)
 
         acc = [accs.tile([P, D], F32, name="acc%d" % i) for i in range(TILES)]
 
@@ -288,7 +276,9 @@ def tile_quantuminspiredneuralcore_pb_k_kernel(
         e_op = {0: quantise_e(copy_e(e_planes[0]))}
         e_planes[1] = planes_of(1)
         w_grp_of = {}
-        for t in range(STEPS + 1):
+        w_op = {}
+
+        def stream_round(t):
             if t % E_LOAD_STEPS == 0 and t // E_LOAD_STEPS + E_AHEAD < E_LOADS:
                 e_raw_of[t // E_LOAD_STEPS + E_AHEAD] = load_e(t // E_LOAD_STEPS + E_AHEAD)
             if t + W_AHEAD < STEPS:
@@ -296,7 +286,7 @@ def tile_quantuminspiredneuralcore_pb_k_kernel(
             if t + 2 < STEPS:
                 e_planes[t + 2] = planes_of(t + 2)
             if t >= 1:
-                w_op = quantise_weights(w_grp_of[t - 1], w_quant)
+                w_op[t - 1] = quantise_weights(w_grp_of[t - 1], w_quant)
             if t + 1 < STEPS:
                 e_grp = copy_e(e_planes[t + 1])
             if t < STEPS:
@@ -304,9 +294,21 @@ def tile_quantuminspiredneuralcore_pb_k_kernel(
             if t + 1 < STEPS:
                 e_op[t + 1] = quantise_e(e_grp)
             if t >= 1:
-                multiply(t - 1, e_op[t - 1], w_op)
+                multiply(t - 1, e_op[t - 1], w_op[t - 1])
 
-        def centre_and_scale(x, x_sum, gain_row, label):
+        for t in range(STEPS - 1):
+            stream_round(t)
+        ln3_g_bank = spread(LN3_G, "ln3_g_bank")
+        ln3_b_bank = spread(LN3_B, "ln3_b_bank")
+        shift_bank = spread(SHIFT, "shift_bank")
+        mod_bank = [spread(MOD + w, "mod_bank%d" % w) for w in range(2)]
+        stream_round(STEPS - 1)
+        stream_round(STEPS)
+        nc.scalar.activation(out=table_warm[:], in_=eps[:], func=ACT.Sqrt)
+        ln3_g_row = to_sbuf(ln3_g_bank, "ln3_g_row")
+        ln3_b_row = to_sbuf(ln3_b_bank, "ln3_b_row")
+
+        def row_stats(x, x_sum, label):
             neg_mean = small.tile([P, 1], F32, name="neg_mean" + label)
             nc.vector.tensor_scalar(
                 out=neg_mean[:], in0=x_sum[:], scalar1=-1.0 / D, scalar2=None, op0=ALU.mult
@@ -316,17 +318,23 @@ def tile_quantuminspiredneuralcore_pb_k_kernel(
             nc.scalar.activation(
                 out=squares[:], in_=x[:], func=ACT.Square, bias=neg_mean[:, 0:1], accum_out=sum_sq[:]
             )
+            return neg_mean, sum_sq
+
+        def centre(x, neg_mean, gain_row, label):
             centred = work.tile([P, D], F32, name="centred" + label)
             nc.vector.scalar_tensor_tensor(
                 out=centred[:], in0=x[:], scalar=neg_mean[:, 0:1], in1=gain_row[:], op0=ALU.add, op1=ALU.mult
             )
+            return centred
+
+        def inverse_std(sum_sq, label):
             std = small.tile([P, 1], F32, name="std" + label)
             nc.scalar.activation(
                 out=std[:], in_=sum_sq[:], func=ACT.Sqrt, bias=eps[:, 0:1], scale=1.0 / D
             )
             rstd = small.tile([P, 1], F32, name="rstd" + label)
             nc.vector.reciprocal(out=rstd[:], in_=std[:])
-            return centred, rstd
+            return rstd
 
         def scale_and_shift(centred, rstd, shift, name):
             result = work.tile([P, D], F32, name=name)
@@ -335,26 +343,28 @@ def tile_quantuminspiredneuralcore_pb_k_kernel(
             )
             return result
 
-        def first_norm(i):
-            x = work.tile([P, D], F32, name="x%d" % i)
-            x_sum = small.tile([P, 1], F32, name="x_sum%d" % i)
+        def add_rows(in0, in1, name):
+            total = work.tile([P, D], F32, name=name)
+            total_sum = small.tile([P, 1], F32, name=name + "_sum")
             nc.vector.scalar_tensor_tensor(
-                out=x[:], in0=acc[i][:], scalar=1.0, in1=h_bias[:, i, :], op0=ALU.mult, op1=ALU.add,
-                accum_out=x_sum[:],
+                out=total[:], in0=in0, scalar=1.0, in1=in1, op0=ALU.mult, op1=ALU.add, accum_out=total_sum[:]
             )
-            centred, rstd = centre_and_scale(x, x_sum, ln3_g_row, "_a%d" % i)
-            hn = scale_and_shift(centred, rstd, ln3_b_row, "hn%d" % i)
-            hn_shifted = scale_and_shift(centred, rstd, shift_row, "hn_shifted%d" % i)
-            return hn, hn_shifted
+            return total, total_sum
 
-        def pathways(i, hn):
+        def transpose_hn(hn):
             hn_bank = banks.tile([P, PACK, P], F32, name="hn_bank", tag="bank")
             for t in range(PACK):
                 nc.tensor.transpose(
                     out=hn_bank[:, t, :], in_=hn[:, t * P : (t + 1) * P], identity=ident_f32[:]
                 )
+            return hn_bank
+
+        def round_hn(i, hn_bank):
             hn_grp = work.tile([P, P, PACK], BF16, name="hn_grp%d" % i, align_bytes=64)
             nc.scalar.copy(out=hn_grp[:], in_=hn_bank[:].rearrange("p t r -> p r t"))
+            return hn_grp
+
+        def pathways(i, hn_grp):
             hn_codes = work.tile([P, P], U32, name="hn_codes%d" % i, align_bytes=64)
             hn_scales = work.tile([P, P], U8, name="hn_scales%d" % i, align_bytes=64)
             nc.vector.quantize_mx(
@@ -378,23 +388,40 @@ def tile_quantuminspiredneuralcore_pb_k_kernel(
                 products.append(product)
             return products
 
-        def second_norm(i, hn_shifted, products):
-            first = work.tile([P, D], F32, name="first%d" % i)
-            nc.vector.tensor_tensor(out=first[:], in0=products[0][:], in1=mod_row[0][:], op=ALU.mult)
-            second = work.tile([P, D], F32, name="second%d" % i)
-            nc.vector.tensor_tensor(out=second[:], in0=products[1][:], in1=mod_row[1][:], op=ALU.mult)
-            nc.vector.tensor_tensor(out=first[:], in0=first[:], in1=hn_shifted[:], op=ALU.add)
-            y = work.tile([P, D], F32, name="y%d" % i)
-            y_sum = small.tile([P, 1], F32, name="y_sum%d" % i)
-            nc.vector.scalar_tensor_tensor(
-                out=y[:], in0=first[:], scalar=1.0, in1=second[:], op0=ALU.mult, op1=ALU.add,
-                accum_out=y_sum[:],
-            )
-            centred, rstd = centre_and_scale(y, y_sum, ln4_g_row, "_b%d" % i)
-            result = scale_and_shift(centred, rstd, ln4_b_row, "result%d" % i)
-            nc.sync.dma_start(out=out[i], in_=result[:])
+        def weigh(i, w, product):
+            weighted = work.tile([P, D], F32, name="weighted%d_%d" % (w, i))
+            nc.vector.tensor_tensor(out=weighted[:], in0=product[:], in1=mod_row[w][:], op=ALU.mult)
+            return weighted
 
-        normed = [first_norm(i) for i in range(TILES)]
-        products = [pathways(i, normed[i][0]) for i in range(TILES)]
-        for i in range(TILES):
-            second_norm(i, normed[i][1], products[i])
+        both = range(TILES)
+        x = [add_rows(acc[i][:], h_bias[:, i, :], "x%d" % i) for i in both]
+        stats = [row_stats(x[i][0], x[i][1], "_a%d" % i) for i in both]
+        centred = [centre(x[i][0], stats[i][0], ln3_g_row, "_a%d" % i) for i in both]
+        rstd = [inverse_std(stats[i][1], "_a%d" % i) for i in both]
+        hn = [scale_and_shift(centred[i], rstd[i], ln3_b_row, "hn%d" % i) for i in both]
+        hn_bank = [transpose_hn(hn[i]) for i in both]
+        ln4_g_bank = spread(LN4_G, "ln4_g_bank")
+        ln4_b_bank = spread(LN4_B, "ln4_b_bank")
+        shift_row = to_sbuf(shift_bank, "shift_row")
+        mod_row = [to_sbuf(mod_bank[w], "mod_row%d" % w) for w in range(2)]
+        hn_grp = [round_hn(i, hn_bank[i]) for i in both]
+        ln4_g_row = to_sbuf(ln4_g_bank, "ln4_g_row")
+        ln4_b_row = to_sbuf(ln4_b_bank, "ln4_b_row")
+        hn_shifted = []
+        for i in both:
+            shifted = work.tile([P, D], F32, name="hn_shifted%d" % i)
+            nc.gpsimd.tensor_tensor(out=shifted[:], in0=hn[i][:], in1=shift_row[:], op=ALU.add)
+            hn_shifted.append(shifted)
+        products = [pathways(i, hn_grp[i]) for i in both]
+        weighted = [[weigh(i, w, products[i][w]) for w in range(2)] for i in both]
+        for i in both:
+            nc.gpsimd.tensor_tensor(
+                out=hn_shifted[i][:], in0=hn_shifted[i][:], in1=weighted[i][0][:], op=ALU.add
+            )
+        y = [add_rows(weighted[i][1][:], hn_shifted[i][:], "y%d" % i) for i in both]
+        stats = [row_stats(y[i][0], y[i][1], "_b%d" % i) for i in both]
+        centred = [centre(y[i][0], stats[i][0], ln4_g_row, "_b%d" % i) for i in both]
+        rstd = [inverse_std(stats[i][1], "_b%d" % i) for i in both]
+        for i in both:
+            result = scale_and_shift(centred[i], rstd[i], ln4_b_row, "result%d" % i)
+            nc.sync.dma_start(out=out[i], in_=result[:])

@@ -24,6 +24,9 @@ STEP_PASSES = 2
 STEPS = K // (STEP_PASSES * K_PASS)
 E_LOAD_STEPS = 2
 E_LOADS = STEPS // E_LOAD_STEPS
+PIECES = [(s * STEP_PASSES, STEP_PASSES) for s in range(STEPS - 1)] + [
+    (K // K_PASS - STEP_PASSES + c, 1) for c in range(STEP_PASSES)
+]
 W_AHEAD = 4
 E_AHEAD = 2
 
@@ -62,12 +65,13 @@ def tile_quantuminspiredneuralcore_pb_k_kernel(
         banks = ctx.enter_context(tc.psum_pool(name="banks", bufs=6))
 
         def load_weight_rows(view):
-            w_raw = w_raws.tile([P, STEP_PASSES, PACK, D], BF16, name="w_raw", tag="w_raw")
+            w_raw = w_raws.tile(list(view.shape), BF16, name="w_raw", tag="w_raw")
             nc.sync.dma_start(out=w_raw[:], in_=view)
             return w_raw
 
-        def load_w(step):
-            rows = ent_pw[step * STEP_PASSES * K_PASS : (step + 1) * STEP_PASSES * K_PASS, :]
+        def load_w(piece):
+            first_pass, passes = PIECES[piece]
+            rows = ent_pw[first_pass * K_PASS : (first_pass + passes) * K_PASS, :]
             return load_weight_rows(rows.rearrange("(c p t) n -> p c t n", p=P, t=PACK))
 
         def load_e(load):
@@ -80,14 +84,13 @@ def tile_quantuminspiredneuralcore_pb_k_kernel(
             return e_raw
 
         def regroup_weights(w_raw):
-            w_grp = grouped.tile(
-                [P, STEP_PASSES, D, PACK], BF16, name="w_grp", tag="w_grp", align_bytes=64
-            )
+            passes = w_raw.shape[1]
+            w_grp = grouped.tile([P, passes, D, PACK], BF16, name="w_grp", tag="w_grp", align_bytes=64)
             nc.vector.tensor_copy(
                 out=w_grp[:, :, 0:V_COLS, :].rearrange("p c (a i) t -> p c a t i", i=4),
                 in_=w_raw[:, :, :, 0:V_COLS].rearrange("p c t (a i) -> p c a t i", i=4),
             )
-            for c in range(STEP_PASSES):
+            for c in range(passes):
                 nc.scalar.copy(
                     out=w_grp[:, c, V_COLS:D, :].rearrange("p (a i) t -> p a t i", i=4),
                     in_=w_raw[:, c, :, V_COLS:D].rearrange("p t (a i) -> p a t i", i=4),
@@ -95,8 +98,9 @@ def tile_quantuminspiredneuralcore_pb_k_kernel(
             return w_grp
 
         def quantise_weights(w_grp, pool):
-            codes = pool.tile([P, STEP_PASSES * D], U32, name="w_codes", tag="w_codes", align_bytes=64)
-            scales = pool.tile([P, STEP_PASSES * D], U8, name="w_scales", tag="w_scales", align_bytes=64)
+            passes = w_grp.shape[1]
+            codes = pool.tile([P, passes * D], U32, name="w_codes", tag="w_codes", align_bytes=64)
+            scales = pool.tile([P, passes * D], U8, name="w_scales", tag="w_scales", align_bytes=64)
             nc.vector.quantize_mx(
                 out=codes[:].bitcast(FP8X4),
                 scales=scales[:],
@@ -143,14 +147,16 @@ def tile_quantuminspiredneuralcore_pb_k_kernel(
             )
             return codes, scales
 
-        def multiply(step, e_op, w_op):
-            e_codes, e_scales = e_op
-            w_codes, w_scales = w_op
-            for c in range(STEP_PASSES):
-                k_pass = step * STEP_PASSES + c
+        def multiply(piece):
+            first_pass, passes = PIECES[piece]
+            e_codes, e_scales = e_op[first_pass // STEP_PASSES]
+            w_codes, w_scales = w_op[piece]
+            for c in range(passes):
+                k_pass = first_pass + c
                 w_cols = slice(c * D, (c + 1) * D)
                 for i in range(TILES):
-                    e_cols = slice((i * STEP_PASSES + c) * P, (i * STEP_PASSES + c + 1) * P)
+                    e_first = (i * STEP_PASSES + k_pass % STEP_PASSES) * P
+                    e_cols = slice(e_first, e_first + P)
                     nc.tensor.matmul_mx(
                         out=acc[i][:],
                         lhsT=e_codes[:, e_cols].bitcast(FP8X4),
@@ -174,7 +180,7 @@ def tile_quantuminspiredneuralcore_pb_k_kernel(
             (LN4_G, ln4_g.rearrange("(o d) -> o d", o=1)),
             (LN4_B, ln4_b.rearrange("(o d) -> o d", o=1)),
         ):
-            nc.sync.dma_start(out=vec_rows[row : row + vector.shape[0], :], in_=vector)
+            nc.scalar.dma_start(out=vec_rows[row : row + vector.shape[0], :], in_=vector)
         h_sb = consts.tile([P, TILES, D], BF16, name="h_sb")
         nc.scalar.dma_start(out=h_sb[:], in_=h.rearrange("b s d -> s b d"))
 
@@ -182,8 +188,8 @@ def tile_quantuminspiredneuralcore_pb_k_kernel(
         e_raw_of = {0: load_e(0)}
         w_raw_of = {0: load_w(0)}
         e_raw_of[1] = load_e(1)
-        for step in range(1, W_AHEAD):
-            w_raw_of[step] = load_w(step)
+        for piece in range(1, W_AHEAD):
+            w_raw_of[piece] = load_w(piece)
 
         ident_bf16 = consts.tile([P, P], BF16, name="ident_bf16")
         masks.make_identity(nc, ident_bf16[:])
@@ -261,6 +267,12 @@ def tile_quantuminspiredneuralcore_pb_k_kernel(
         nc.vector.tensor_tensor(
             out=cols[:, :, SHIFT : SHIFT + 1], in0=weighted_b[:, :, 0:1], in1=weighted_b[:, :, 1:2], op=ALU.add
         )
+        nc.vector.tensor_tensor(
+            out=cols[:, :, SHIFT : SHIFT + 1],
+            in0=cols[:, :, SHIFT : SHIFT + 1],
+            in1=cols[:, :, LN3_B : LN3_B + 1],
+            op=ALU.add,
+        )
         h_bias = consts.tile([P, TILES, D], F32, name="h_bias")
         for i in range(TILES):
             nc.vector.tensor_tensor(out=h_bias[:, i, :], in0=bias_bank[:], in1=h_sb[:, i, :], op=ALU.add)
@@ -281,7 +293,7 @@ def tile_quantuminspiredneuralcore_pb_k_kernel(
         def stream_round(t):
             if t % E_LOAD_STEPS == 0 and t // E_LOAD_STEPS + E_AHEAD < E_LOADS:
                 e_raw_of[t // E_LOAD_STEPS + E_AHEAD] = load_e(t // E_LOAD_STEPS + E_AHEAD)
-            if t + W_AHEAD < STEPS:
+            if t + W_AHEAD < len(PIECES):
                 w_raw_of[t + W_AHEAD] = load_w(t + W_AHEAD)
             if t + 2 < STEPS:
                 e_planes[t + 2] = planes_of(t + 2)
@@ -289,12 +301,12 @@ def tile_quantuminspiredneuralcore_pb_k_kernel(
                 w_op[t - 1] = quantise_weights(w_grp_of[t - 1], w_quant)
             if t + 1 < STEPS:
                 e_grp = copy_e(e_planes[t + 1])
-            if t < STEPS:
+            if t < len(PIECES):
                 w_grp_of[t] = regroup_weights(w_raw_of[t])
             if t + 1 < STEPS:
                 e_op[t + 1] = quantise_e(e_grp)
             if t >= 1:
-                multiply(t - 1, e_op[t - 1], w_op[t - 1])
+                multiply(t - 1)
 
         for t in range(STEPS - 1):
             stream_round(t)
@@ -302,8 +314,8 @@ def tile_quantuminspiredneuralcore_pb_k_kernel(
         ln3_b_bank = spread(LN3_B, "ln3_b_bank")
         shift_bank = spread(SHIFT, "shift_bank")
         mod_bank = [spread(MOD + w, "mod_bank%d" % w) for w in range(2)]
-        stream_round(STEPS - 1)
-        stream_round(STEPS)
+        for t in range(STEPS - 1, len(PIECES) + 1):
+            stream_round(t)
         nc.scalar.activation(out=table_warm[:], in_=eps[:], func=ACT.Sqrt)
         ln3_g_row = to_sbuf(ln3_g_bank, "ln3_g_row")
         ln3_b_row = to_sbuf(ln3_b_bank, "ln3_b_row")
@@ -400,19 +412,13 @@ def tile_quantuminspiredneuralcore_pb_k_kernel(
         rstd = [inverse_std(stats[i][1], "_a%d" % i) for i in both]
         hn = [scale_and_shift(centred[i], rstd[i], ln3_b_row, "hn%d" % i) for i in both]
         hn_bank = [transpose_hn(hn[i]) for i in both]
-        ln4_g_bank = spread(LN4_G, "ln4_g_bank")
-        ln4_b_bank = spread(LN4_B, "ln4_b_bank")
         shift_row = to_sbuf(shift_bank, "shift_row")
-        mod_row = [to_sbuf(mod_bank[w], "mod_row%d" % w) for w in range(2)]
         hn_grp = [round_hn(i, hn_bank[i]) for i in both]
-        ln4_g_row = to_sbuf(ln4_g_bank, "ln4_g_row")
-        ln4_b_row = to_sbuf(ln4_b_bank, "ln4_b_row")
-        hn_shifted = []
-        for i in both:
-            shifted = work.tile([P, D], F32, name="hn_shifted%d" % i)
-            nc.gpsimd.tensor_tensor(out=shifted[:], in0=hn[i][:], in1=shift_row[:], op=ALU.add)
-            hn_shifted.append(shifted)
+        mod_row = [to_sbuf(mod_bank[w], "mod_row%d" % w) for w in range(2)]
+        hn_shifted = [scale_and_shift(centred[i], rstd[i], shift_row, "hn_shifted%d" % i) for i in both]
         products = [pathways(i, hn_grp[i]) for i in both]
+        ln4_g_row = to_sbuf(spread(LN4_G, "ln4_g_bank"), "ln4_g_row")
+        ln4_b_row = to_sbuf(spread(LN4_B, "ln4_b_bank"), "ln4_b_row")
         weighted = [[weigh(i, w, products[i][w]) for w in range(2)] for i in both]
         for i in both:
             nc.gpsimd.tensor_tensor(

@@ -22,23 +22,24 @@ EPS = 1e-5
 
 STEP_PASSES = 2
 STEPS = K // (STEP_PASSES * K_PASS)
-E_LOAD_STEPS = 2
-E_LOADS = STEPS // E_LOAD_STEPS
-PIECES = [(s * STEP_PASSES, STEP_PASSES) for s in range(STEPS - 1)] + [
-    (K // K_PASS - STEP_PASSES + c, 1) for c in range(STEP_PASSES)
-]
-W_AHEAD = 4
-E_AHEAD = 2
+PIECES = (
+    [(c, 1) for c in range(STEP_PASSES)]
+    + [(s * STEP_PASSES, STEP_PASSES) for s in range(1, STEPS - 1)]
+    + [(K // K_PASS - STEP_PASSES + c, 1) for c in range(STEP_PASSES)]
+)
+AHEAD = 5
+PATH_ROUND = 6
 
 V_COLS = 288
 
 FLOPS = 2 * TILES * P * K * D + 2 * 2 * TILES * P * D * D
 
-ENT_PB, LN3_G, LN3_B, PATH_B, PHASE, LN4_G, LN4_B = 0, 1, 2, 3, 5, 7, 8
-LOADED = 9
-MOD = 9
-SHIFT = 11
-COLUMNS = 12
+PATH_B, PHASE = 0, 2
+LOADED = 4
+MOD = 4
+SHIFT = 6
+COLUMNS = 7
+ENT_PB, LN3_G, LN3_B, LN4_G, LN4_B = range(5)
 
 TWO_PI_HI = 6.28125
 TWO_PI_MID = 0.0019353071693331003
@@ -54,8 +55,8 @@ def tile_quantuminspiredneuralcore_pb_k_kernel(
     nc = tc.nc
     with ExitStack() as ctx:
         consts = ctx.enter_context(tc.tile_pool(name="consts", bufs=1))
-        e_raws = ctx.enter_context(tc.tile_pool(name="e_raws", bufs=E_AHEAD + 1))
-        w_raws = ctx.enter_context(tc.tile_pool(name="w_raws", bufs=W_AHEAD + 1))
+        e_raws = ctx.enter_context(tc.tile_pool(name="e_raws", bufs=AHEAD + 2))
+        w_raws = ctx.enter_context(tc.tile_pool(name="w_raws", bufs=AHEAD + 2))
         grouped = ctx.enter_context(tc.tile_pool(name="grouped", bufs=3))
         w_quant = ctx.enter_context(tc.tile_pool(name="w_quant", bufs=3))
         e_quant = ctx.enter_context(tc.tile_pool(name="e_quant", bufs=4))
@@ -74,12 +75,12 @@ def tile_quantuminspiredneuralcore_pb_k_kernel(
             rows = ent_pw[first_pass * K_PASS : (first_pass + passes) * K_PASS, :]
             return load_weight_rows(rows.rearrange("(c p t) n -> p c t n", p=P, t=PACK))
 
-        def load_e(load):
-            width = E_LOAD_STEPS * STEP_PASSES * K_PASS
+        def load_e(step):
+            width = STEP_PASSES * K_PASS
             e_raw = e_raws.tile([P, TILES, width], BF16, name="e_raw", tag="e_raw")
             nc.sync.dma_start(
                 out=e_raw[:],
-                in_=e[:, :, load * width : (load + 1) * width].rearrange("b s k -> s b k"),
+                in_=e[:, :, step * width : (step + 1) * width].rearrange("b s k -> s b k"),
             )
             return e_raw
 
@@ -108,14 +109,14 @@ def tile_quantuminspiredneuralcore_pb_k_kernel(
             )
             return codes, scales
 
-        def transpose_e(e_raw, half):
+        def transpose_e(e_raw):
             words = K_PASS // 2
             planes = []
             for i in range(TILES):
                 e_words = e_raw[:, i, :].bitcast(F32)
                 bank = banks.tile([P, STEP_PASSES, 2, P], F32, name="e_bank", tag="bank")
                 for c in range(STEP_PASSES):
-                    first = (half * STEP_PASSES + c) * words
+                    first = c * words
                     for u in range(2):
                         nc.tensor.transpose(
                             out=bank[:, c, u, :],
@@ -169,61 +170,63 @@ def tile_quantuminspiredneuralcore_pb_k_kernel(
 
         ctx.enter_context(tc.manual_schedule())
 
+        path_rows = consts.tile([P, D], BF16, name="path_rows")
+        nc.vector.memset(path_rows[:].bitcast(mybir.dt.int32), 0)
+        eps = consts.tile([P, 1], F32, name="eps")
+        nc.vector.memset(eps[:], EPS)
         vec_rows = consts.tile([P, D], BF16, name="vec_rows")
-        nc.vector.memset(vec_rows[:], 0.0)
-        for row, vector in (
-            (PHASE, phase),
-            (PATH_B, path_b),
-            (ENT_PB, ent_pb.rearrange("(o d) -> o d", o=1)),
-            (LN3_G, ln3_g.rearrange("(o d) -> o d", o=1)),
-            (LN3_B, ln3_b.rearrange("(o d) -> o d", o=1)),
-            (LN4_G, ln4_g.rearrange("(o d) -> o d", o=1)),
-            (LN4_B, ln4_b.rearrange("(o d) -> o d", o=1)),
-        ):
-            nc.scalar.dma_start(out=vec_rows[row : row + vector.shape[0], :], in_=vector)
-        h_sb = consts.tile([P, TILES, D], BF16, name="h_sb")
-        nc.scalar.dma_start(out=h_sb[:], in_=h.rearrange("b s d -> s b d"))
 
-        path_raw = load_weight_rows(path_w.rearrange("w (t p) n -> p w t n", p=P))
-        e_raw_of = {0: load_e(0)}
-        w_raw_of = {0: load_w(0)}
-        e_raw_of[1] = load_e(1)
-        for piece in range(1, W_AHEAD):
-            w_raw_of[piece] = load_w(piece)
+        def as_row(vector):
+            return vector.rearrange("(o d) -> o d", o=1)
+
+        for row, vector in ((PHASE, phase), (PATH_B, path_b)):
+            nc.sync.dma_start(out=path_rows[row : row + vector.shape[0], :], in_=vector)
+
+        e_raw_of = {}
+        w_raw_of = {}
+
+        def load_for_round(t):
+            if t < STEPS:
+                e_raw_of[t] = load_e(t)
+            if t < len(PIECES):
+                w_raw_of[t] = load_w(t)
+
+        for t in range(AHEAD):
+            load_for_round(t)
 
         ident_bf16 = consts.tile([P, P], BF16, name="ident_bf16")
         masks.make_identity(nc, ident_bf16[:])
         ident_f32 = consts.tile([P, P], F32, name="ident_f32")
         masks.make_identity(nc, ident_f32[:])
-        eps = consts.tile([P, 1], F32, name="eps")
-        nc.vector.memset(eps[:], EPS)
+        nc.gpsimd.memset(vec_rows[:], 0.0)
         table_warm = consts.tile([P, 1], F32, name="table_warm")
         nc.scalar.activation(out=table_warm[:], in_=eps[:], func=ACT.Sin)
 
         vec_bank = banks.tile([P, SLICES, P], BF16, name="vec_bank", tag="bank")
         for s in range(SLICES):
             nc.tensor.transpose(
-                out=vec_bank[:, s, :], in_=vec_rows[:, s * P : (s + 1) * P], identity=ident_bf16[:]
+                out=vec_bank[:, s, :], in_=path_rows[:, s * P : (s + 1) * P], identity=ident_bf16[:]
             )
         cols = consts.tile([P, SLICES, COLUMNS], F32, name="cols")
         nc.vector.tensor_copy(out=cols[:, :, 0:LOADED], in_=vec_bank[:, :, 0:LOADED])
 
-        def spread(column, name):
+        def spread_row(row, name, plus=None):
             bank = banks.tile([P, D], F32, name=name, tag="bank")
-            for s in range(SLICES):
-                nc.tensor.transpose(
-                    out=bank[:, s * P : (s + 1) * P],
-                    in_=cols[:, s, column : column + 1].to_broadcast([P, P]),
-                    identity=ident_f32[:],
-                )
+            if plus is not None:
+                nc.tensor.matmul(out=bank[:], lhsT=ident_bf16[:], rhs=plus, start=True, stop=False)
+            nc.tensor.matmul(
+                out=bank[:],
+                lhsT=ident_bf16[:, row : row + 1].to_broadcast([P, P]),
+                rhs=vec_rows[:],
+                start=plus is None,
+                stop=True,
+            )
             return bank
 
         def to_sbuf(bank, name):
             row = consts.tile([P, D], F32, name=name)
             nc.scalar.copy(out=row[:], in_=bank[:])
             return row
-
-        bias_bank = spread(ENT_PB, "bias_bank")
 
         phases = cols[:, :, PHASE : PHASE + 2]
         turns = consts.tile([P, SLICES, 2], F32, name="turns")
@@ -248,8 +251,7 @@ def tile_quantuminspiredneuralcore_pb_k_kernel(
         nc.scalar.activation(out=sin_full[:], in_=angle[:], func=ACT.Sin)
         sin_half = consts.tile([P, SLICES, 2], F32, name="sin_half")
         nc.scalar.activation(out=sin_half[:], in_=angle[:], func=ACT.Sin, scale=0.5)
-
-        path_grp = regroup_weights(path_raw)
+        nc.scalar.activation(out=table_warm[:], in_=eps[:], func=ACT.Abs_reciprocal_sqrt)
 
         half_sq = consts.tile([P, SLICES, 2], F32, name="half_sq")
         nc.vector.tensor_tensor(out=half_sq[:], in0=sin_half[:], in1=sin_half[:], op=ALU.mult)
@@ -267,70 +269,84 @@ def tile_quantuminspiredneuralcore_pb_k_kernel(
         nc.vector.tensor_tensor(
             out=cols[:, :, SHIFT : SHIFT + 1], in0=weighted_b[:, :, 0:1], in1=weighted_b[:, :, 1:2], op=ALU.add
         )
-        nc.vector.tensor_tensor(
-            out=cols[:, :, SHIFT : SHIFT + 1],
-            in0=cols[:, :, SHIFT : SHIFT + 1],
-            in1=cols[:, :, LN3_B : LN3_B + 1],
-            op=ALU.add,
-        )
-        h_bias = consts.tile([P, TILES, D], F32, name="h_bias")
-        for i in range(TILES):
-            nc.vector.tensor_tensor(out=h_bias[:, i, :], in0=bias_bank[:], in1=h_sb[:, i, :], op=ALU.add)
 
-        path_op = quantise_weights(path_grp, consts)
-
-        acc = [accs.tile([P, D], F32, name="acc%d" % i) for i in range(TILES)]
+        acc = [accs.tile([P, D], F32, name="acc%d" % i, tag="acc%d" % i) for i in range(TILES)]
 
         def planes_of(step):
-            return transpose_e(e_raw_of[step // E_LOAD_STEPS], step % E_LOAD_STEPS)
+            return transpose_e(e_raw_of[step])
 
         e_planes = {0: planes_of(0)}
-        e_op = {0: quantise_e(copy_e(e_planes[0]))}
-        e_planes[1] = planes_of(1)
+        e_grp_of = {}
+        e_op = {}
         w_grp_of = {}
         w_op = {}
 
         def stream_round(t):
-            if t % E_LOAD_STEPS == 0 and t // E_LOAD_STEPS + E_AHEAD < E_LOADS:
-                e_raw_of[t // E_LOAD_STEPS + E_AHEAD] = load_e(t // E_LOAD_STEPS + E_AHEAD)
-            if t + W_AHEAD < len(PIECES):
-                w_raw_of[t + W_AHEAD] = load_w(t + W_AHEAD)
-            if t + 2 < STEPS:
-                e_planes[t + 2] = planes_of(t + 2)
+            load_for_round(t + AHEAD)
+            if t + 1 < STEPS:
+                e_planes[t + 1] = planes_of(t + 1)
+            if t < STEPS:
+                e_grp_of[t] = copy_e(e_planes[t])
+            if 1 <= t <= STEPS:
+                e_op[t - 1] = quantise_e(e_grp_of[t - 1])
             if t >= 1:
                 w_op[t - 1] = quantise_weights(w_grp_of[t - 1], w_quant)
-            if t + 1 < STEPS:
-                e_grp = copy_e(e_planes[t + 1])
             if t < len(PIECES):
                 w_grp_of[t] = regroup_weights(w_raw_of[t])
-            if t + 1 < STEPS:
-                e_op[t + 1] = quantise_e(e_grp)
             if t >= 1:
                 multiply(t - 1)
 
-        for t in range(STEPS - 1):
+        def load_vectors(*rows):
+            for row, vector in rows:
+                nc.sync.dma_start(out=vec_rows[row : row + 1, :], in_=as_row(vector))
+
+        for t in range(PATH_ROUND - AHEAD):
             stream_round(t)
-        ln3_g_bank = spread(LN3_G, "ln3_g_bank")
-        ln3_b_bank = spread(LN3_B, "ln3_b_bank")
-        shift_bank = spread(SHIFT, "shift_bank")
-        mod_bank = [spread(MOD + w, "mod_bank%d" % w) for w in range(2)]
-        for t in range(STEPS - 1, len(PIECES) + 1):
+        path_raw = load_weight_rows(path_w.rearrange("w (p t) n -> p w t n", t=PACK))
+        load_vectors((ENT_PB, ent_pb))
+        h_sb = consts.tile([P, TILES, D], BF16, name="h_sb")
+        nc.sync.dma_start(out=h_sb[:], in_=h.rearrange("b s d -> s b d"))
+        for t in range(PATH_ROUND - AHEAD, PATH_ROUND):
             stream_round(t)
-        nc.scalar.activation(out=table_warm[:], in_=eps[:], func=ACT.Sqrt)
+        path_grp = regroup_weights(path_raw)
+        stream_round(PATH_ROUND)
+        path_op = quantise_weights(path_grp, consts)
+        load_vectors((LN3_G, ln3_g), (LN3_B, ln3_b))
+        stream_round(PATH_ROUND + 1)
+        load_vectors((LN4_G, ln4_g), (LN4_B, ln4_b))
+        for t in range(PATH_ROUND + 2, STEPS):
+            stream_round(t)
+        h_bias_bank = [spread_row(ENT_PB, "h_bias_bank%d" % i, plus=h_sb[:, i, :]) for i in range(TILES)]
+        ln3_g_bank = spread_row(LN3_G, "ln3_g_bank")
+        ln3_b_bank = spread_row(LN3_B, "ln3_b_bank")
+        ln4_g_bank = spread_row(LN4_G, "ln4_g_bank")
+        ln4_b_bank = spread_row(LN4_B, "ln4_b_bank")
+        for t in range(STEPS, len(PIECES) + 1):
+            stream_round(t)
+        h_bias = [to_sbuf(h_bias_bank[i], "h_bias%d" % i) for i in range(TILES)]
         ln3_g_row = to_sbuf(ln3_g_bank, "ln3_g_row")
         ln3_b_row = to_sbuf(ln3_b_bank, "ln3_b_row")
+        ln4_g_row = to_sbuf(ln4_g_bank, "ln4_g_row")
+        ln4_b_row = to_sbuf(ln4_b_bank, "ln4_b_row")
 
-        def row_stats(x, x_sum, label):
+        def inverse_std(x, x_sum, label):
+            squares = work.tile([P, D], F32, name="squares" + label)
+            sum_sq = small.tile([P, 1], F32, name="sum_sq" + label)
+            nc.scalar.activation(
+                out=squares[:], in_=x[:], func=ACT.Square, scale=-float(D), bias=x_sum[:, 0:1], accum_out=sum_sq[:]
+            )
+            rstd = small.tile([P, 1], F32, name="rstd" + label)
+            nc.scalar.activation(
+                out=rstd[:], in_=sum_sq[:], func=ACT.Abs_reciprocal_sqrt, bias=eps[:, 0:1], scale=1.0 / D**3
+            )
+            return rstd
+
+        def negative_mean(x_sum, label):
             neg_mean = small.tile([P, 1], F32, name="neg_mean" + label)
             nc.vector.tensor_scalar(
                 out=neg_mean[:], in0=x_sum[:], scalar1=-1.0 / D, scalar2=None, op0=ALU.mult
             )
-            squares = work.tile([P, D], F32, name="squares" + label)
-            sum_sq = small.tile([P, 1], F32, name="sum_sq" + label)
-            nc.scalar.activation(
-                out=squares[:], in_=x[:], func=ACT.Square, bias=neg_mean[:, 0:1], accum_out=sum_sq[:]
-            )
-            return neg_mean, sum_sq
+            return neg_mean
 
         def centre(x, neg_mean, gain_row, label):
             centred = work.tile([P, D], F32, name="centred" + label)
@@ -339,17 +355,8 @@ def tile_quantuminspiredneuralcore_pb_k_kernel(
             )
             return centred
 
-        def inverse_std(sum_sq, label):
-            std = small.tile([P, 1], F32, name="std" + label)
-            nc.scalar.activation(
-                out=std[:], in_=sum_sq[:], func=ACT.Sqrt, bias=eps[:, 0:1], scale=1.0 / D
-            )
-            rstd = small.tile([P, 1], F32, name="rstd" + label)
-            nc.vector.reciprocal(out=rstd[:], in_=std[:])
-            return rstd
-
-        def scale_and_shift(centred, rstd, shift, name):
-            result = work.tile([P, D], F32, name=name)
+        def scale_and_shift(centred, rstd, shift, name, dtype=F32):
+            result = work.tile([P, D], dtype, name=name)
             nc.vector.scalar_tensor_tensor(
                 out=result[:], in0=centred[:], scalar=rstd[:, 0:1], in1=shift[:], op0=ALU.mult, op1=ALU.add
             )
@@ -363,71 +370,90 @@ def tile_quantuminspiredneuralcore_pb_k_kernel(
             )
             return total, total_sum
 
-        def transpose_hn(hn):
-            hn_bank = banks.tile([P, PACK, P], F32, name="hn_bank", tag="bank")
-            for t in range(PACK):
+        def transpose_hn(hn_rounded):
+            words = hn_rounded[:].bitcast(F32)
+            hn_bank = banks.tile([P, 2, P], F32, name="hn_bank", tag="bank")
+            for u in range(2):
                 nc.tensor.transpose(
-                    out=hn_bank[:, t, :], in_=hn[:, t * P : (t + 1) * P], identity=ident_f32[:]
+                    out=hn_bank[:, u, :], in_=words[:, u : D // 2 : 2], identity=ident_f32[:]
                 )
             return hn_bank
 
-        def round_hn(i, hn_bank):
-            hn_grp = work.tile([P, P, PACK], BF16, name="hn_grp%d" % i, align_bytes=64)
-            nc.scalar.copy(out=hn_grp[:], in_=hn_bank[:].rearrange("p t r -> p r t"))
+        def group_hn(i, hn_bank):
+            hn_grp = work.tile([P, P * 2], F32, name="hn_grp%d" % i, align_bytes=64)
+            nc.scalar.copy(
+                out=hn_grp[:].rearrange("p (r u) -> p r u", u=2), in_=hn_bank[:].rearrange("p u r -> p r u")
+            )
             return hn_grp
 
-        def pathways(i, hn_grp):
-            hn_codes = work.tile([P, P], U32, name="hn_codes%d" % i, align_bytes=64)
-            hn_scales = work.tile([P, P], U8, name="hn_scales%d" % i, align_bytes=64)
+        def quantise_hn(i, hn_grp):
             nc.vector.quantize_mx(
-                out=hn_codes[:].bitcast(FP8X4),
-                scales=hn_scales[:],
-                in_=hn_grp[:].rearrange("p r t -> p (r t)"),
+                out=hn_codes[:, i * P : (i + 1) * P].bitcast(FP8X4),
+                scales=hn_scales[:, i * P : (i + 1) * P],
+                in_=hn_grp[:].bitcast(BF16),
             )
-            path_codes, path_scales = path_op
-            products = []
-            for w in range(2):
-                product = banks.tile([P, D], F32, name="product", tag="bank")
-                nc.tensor.matmul_mx(
-                    out=product[:],
-                    lhsT=hn_codes[:].bitcast(FP8X4),
-                    lhsT_scale=hn_scales[:],
-                    rhs=path_codes[:, w * D : (w + 1) * D].bitcast(FP8X4),
-                    rhs_scale=path_scales[:, w * D : (w + 1) * D],
-                    start=True,
-                    stop=True,
-                )
-                products.append(product)
-            return products
 
-        def weigh(i, w, product):
-            weighted = work.tile([P, D], F32, name="weighted%d_%d" % (w, i))
-            nc.vector.tensor_tensor(out=weighted[:], in0=product[:], in1=mod_row[w][:], op=ALU.mult)
-            return weighted
+        def pathway(w, f, out):
+            path_codes, path_scales = path_op
+            first = w * D + f * P
+            nc.tensor.matmul_mx(
+                out=out,
+                lhsT=path_codes[:, first : first + P].bitcast(FP8X4),
+                lhsT_scale=path_scales[:, first : first + P],
+                rhs=hn_codes[:].bitcast(FP8X4),
+                rhs_scale=hn_scales[:],
+                start=True,
+                stop=True,
+            )
 
         both = range(TILES)
-        x = [add_rows(acc[i][:], h_bias[:, i, :], "x%d" % i) for i in both]
-        stats = [row_stats(x[i][0], x[i][1], "_a%d" % i) for i in both]
-        centred = [centre(x[i][0], stats[i][0], ln3_g_row, "_a%d" % i) for i in both]
-        rstd = [inverse_std(stats[i][1], "_a%d" % i) for i in both]
+        x = [add_rows(acc[i][:], h_bias[i][:], "x%d" % i) for i in both]
+        rstd = [inverse_std(x[i][0], x[i][1], "_a%d" % i) for i in both]
+        neg_mean = [negative_mean(x[i][1], "_a%d" % i) for i in both]
+        centred = [centre(x[i][0], neg_mean[i], ln3_g_row, "_a%d" % i) for i in both]
+        hn_rounded = [scale_and_shift(centred[i], rstd[i], ln3_b_row, "hn_rounded%d" % i, BF16) for i in both]
+        hn_bank = [transpose_hn(hn_rounded[i]) for i in both]
+        hn_grp = [group_hn(i, hn_bank[i]) for i in both]
         hn = [scale_and_shift(centred[i], rstd[i], ln3_b_row, "hn%d" % i) for i in both]
-        hn_bank = [transpose_hn(hn[i]) for i in both]
-        shift_row = to_sbuf(shift_bank, "shift_row")
-        hn_grp = [round_hn(i, hn_bank[i]) for i in both]
-        mod_row = [to_sbuf(mod_bank[w], "mod_row%d" % w) for w in range(2)]
-        hn_shifted = [scale_and_shift(centred[i], rstd[i], shift_row, "hn_shifted%d" % i) for i in both]
-        products = [pathways(i, hn_grp[i]) for i in both]
-        ln4_g_row = to_sbuf(spread(LN4_G, "ln4_g_bank"), "ln4_g_row")
-        ln4_b_row = to_sbuf(spread(LN4_B, "ln4_b_bank"), "ln4_b_row")
-        weighted = [[weigh(i, w, products[i][w]) for w in range(2)] for i in both]
+        hn_codes = work.tile([P, TILES * P], U32, name="hn_codes", align_bytes=64)
+        hn_scales = work.tile([P, TILES * P], U8, name="hn_scales", align_bytes=64)
         for i in both:
-            nc.gpsimd.tensor_tensor(
-                out=hn_shifted[i][:], in0=hn_shifted[i][:], in1=weighted[i][0][:], op=ALU.add
+            quantise_hn(i, hn_grp[i])
+
+        tokens = TILES * P
+        interf = work.tile([P, SLICES, tokens], F32, name="interf")
+        first_term = work.tile([P, SLICES, tokens], F32, name="first_term")
+        for f in range(SLICES):
+            product = [banks.tile([P, tokens], F32, name="product", tag="bank") for w in range(2)]
+            for w in range(2):
+                pathway(w, f, product[w][:])
+            nc.scalar.activation(
+                out=first_term[:, f, :],
+                in_=product[0][:],
+                func=ACT.Identity,
+                scale=cols[:, f, MOD : MOD + 1],
+                bias=cols[:, f, SHIFT : SHIFT + 1],
             )
-        y = [add_rows(weighted[i][1][:], hn_shifted[i][:], "y%d" % i) for i in both]
-        stats = [row_stats(y[i][0], y[i][1], "_b%d" % i) for i in both]
-        centred = [centre(y[i][0], stats[i][0], ln4_g_row, "_b%d" % i) for i in both]
-        rstd = [inverse_std(stats[i][1], "_b%d" % i) for i in both]
+            nc.vector.scalar_tensor_tensor(
+                out=interf[:, f, :],
+                in0=product[1][:],
+                scalar=cols[:, f, MOD + 1 : MOD + 2],
+                in1=first_term[:, f, :],
+                op0=ALU.mult,
+                op1=ALU.add,
+            )
+        interf_bank = [accs.tile([P, D], F32, name="interf_bank%d" % i, tag="acc%d" % i) for i in both]
+        for i in both:
+            for f in range(SLICES):
+                nc.tensor.transpose(
+                    out=interf_bank[i][:, f * P : (f + 1) * P],
+                    in_=interf[:, f, i * P : (i + 1) * P],
+                    identity=ident_f32[:],
+                )
+        y = [add_rows(interf_bank[i][:], hn[i][:], "y%d" % i) for i in both]
+        rstd = [inverse_std(y[i][0], y[i][1], "_b%d" % i) for i in both]
+        neg_mean = [negative_mean(y[i][1], "_b%d" % i) for i in both]
+        centred = [centre(y[i][0], neg_mean[i], ln4_g_row, "_b%d" % i) for i in both]
         for i in both:
             result = scale_and_shift(centred[i], rstd[i], ln4_b_row, "result%d" % i)
             nc.sync.dma_start(out=out[i], in_=result[:])

@@ -1,3 +1,4 @@
+import math
 from contextlib import ExitStack
 
 import concourse.masks as masks
@@ -28,6 +29,7 @@ PIECES = (
     + [(K // K_PASS - STEP_PASSES + c, 1) for c in range(STEP_PASSES)]
 )
 AHEAD = 5
+E_LOADS = [(0, 1), (1, 1)] + [(s, 2) for s in range(2, STEPS, 2)]
 PATH_ROUND = 6
 
 V_COLS = 288
@@ -35,16 +37,17 @@ V_COLS = 288
 FLOPS = 2 * TILES * P * K * D + 2 * 2 * TILES * P * D * D
 
 PATH_B, PHASE = 0, 2
-LOADED = 4
-MOD = 4
-SHIFT = 6
-COLUMNS = 7
+MOD = 2
+SHIFT = 4
+COLUMNS = 5
 ENT_PB, LN3_G, LN3_B, LN4_G, LN4_B = range(5)
 
 TWO_PI_HI = 6.28125
 TWO_PI_MID = 0.0019353071693331003
 TWO_PI_LO = 1.0253131677018246e-11
 INV_TWO_PI = 0.15915493667125702
+QUARTER_PI = math.pi / 4
+SQRT_2 = math.sqrt(2.0)
 PI_BELOW = 3.141592502593994
 ROUND_MAGIC = 12582912.0
 
@@ -55,7 +58,7 @@ def tile_quantuminspiredneuralcore_pb_k_kernel(
     nc = tc.nc
     with ExitStack() as ctx:
         consts = ctx.enter_context(tc.tile_pool(name="consts", bufs=1))
-        e_raws = ctx.enter_context(tc.tile_pool(name="e_raws", bufs=AHEAD + 2))
+        e_raws = ctx.enter_context(tc.tile_pool(name="e_raws", bufs=AHEAD))
         w_raws = ctx.enter_context(tc.tile_pool(name="w_raws", bufs=AHEAD + 2))
         grouped = ctx.enter_context(tc.tile_pool(name="grouped", bufs=3))
         w_quant = ctx.enter_context(tc.tile_pool(name="w_quant", bufs=3))
@@ -75,14 +78,17 @@ def tile_quantuminspiredneuralcore_pb_k_kernel(
             rows = ent_pw[first_pass * K_PASS : (first_pass + passes) * K_PASS, :]
             return load_weight_rows(rows.rearrange("(c p t) n -> p c t n", p=P, t=PACK))
 
-        def load_e(step):
+        e_raw_of = {}
+
+        def load_e(first_step, steps):
             width = STEP_PASSES * K_PASS
-            e_raw = e_raws.tile([P, TILES, width], BF16, name="e_raw", tag="e_raw")
+            e_raw = e_raws.tile([P, TILES, steps * width], BF16, name="e_raw", tag="e_raw")
             nc.sync.dma_start(
                 out=e_raw[:],
-                in_=e[:, :, step * width : (step + 1) * width].rearrange("b s k -> s b k"),
+                in_=e[:, :, first_step * width : (first_step + steps) * width].rearrange("b s k -> s b k"),
             )
-            return e_raw
+            for s in range(steps):
+                e_raw_of[first_step + s] = (e_raw, s)
 
         def regroup_weights(w_raw):
             passes = w_raw.shape[1]
@@ -109,14 +115,14 @@ def tile_quantuminspiredneuralcore_pb_k_kernel(
             )
             return codes, scales
 
-        def transpose_e(e_raw):
+        def transpose_e(e_raw, step):
             words = K_PASS // 2
             planes = []
             for i in range(TILES):
                 e_words = e_raw[:, i, :].bitcast(F32)
                 bank = banks.tile([P, STEP_PASSES, 2, P], F32, name="e_bank", tag="bank")
                 for c in range(STEP_PASSES):
-                    first = c * words
+                    first = (step * STEP_PASSES + c) * words
                     for u in range(2):
                         nc.tensor.transpose(
                             out=bank[:, c, u, :],
@@ -182,12 +188,12 @@ def tile_quantuminspiredneuralcore_pb_k_kernel(
         for row, vector in ((PHASE, phase), (PATH_B, path_b)):
             nc.sync.dma_start(out=path_rows[row : row + vector.shape[0], :], in_=vector)
 
-        e_raw_of = {}
         w_raw_of = {}
 
         def load_for_round(t):
-            if t < STEPS:
-                e_raw_of[t] = load_e(t)
+            for first_step, steps in E_LOADS:
+                if first_step == t:
+                    load_e(first_step, steps)
             if t < len(PIECES):
                 w_raw_of[t] = load_w(t)
 
@@ -208,7 +214,7 @@ def tile_quantuminspiredneuralcore_pb_k_kernel(
                 out=vec_bank[:, s, :], in_=path_rows[:, s * P : (s + 1) * P], identity=ident_bf16[:]
             )
         cols = consts.tile([P, SLICES, COLUMNS], F32, name="cols")
-        nc.vector.tensor_copy(out=cols[:, :, 0:LOADED], in_=vec_bank[:, :, 0:LOADED])
+        nc.vector.tensor_copy(out=cols[:, :, PATH_B : PATH_B + 2], in_=vec_bank[:, :, PATH_B : PATH_B + 2])
 
         def spread_row(row, name, plus=None):
             bank = banks.tile([P, D], F32, name=name, tag="bank")
@@ -228,17 +234,20 @@ def tile_quantuminspiredneuralcore_pb_k_kernel(
             nc.scalar.copy(out=row[:], in_=bank[:])
             return row
 
-        phases = cols[:, :, PHASE : PHASE + 2]
+        phases = consts.tile([P, SLICES, 2], F32, name="phases")
+        nc.vector.tensor_scalar(
+            out=phases[:], in0=vec_bank[:, :, PHASE : PHASE + 2], scalar1=QUARTER_PI, scalar2=None, op0=ALU.add
+        )
         turns = consts.tile([P, SLICES, 2], F32, name="turns")
         nc.vector.tensor_scalar(
-            out=turns[:], in0=phases, scalar1=INV_TWO_PI, scalar2=ROUND_MAGIC, op0=ALU.mult, op1=ALU.add
+            out=turns[:], in0=phases[:], scalar1=INV_TWO_PI, scalar2=ROUND_MAGIC, op0=ALU.mult, op1=ALU.add
         )
         nc.vector.tensor_scalar(
             out=turns[:], in0=turns[:], scalar1=ROUND_MAGIC, scalar2=None, op0=ALU.subtract
         )
         angle = consts.tile([P, SLICES, 2], F32, name="angle")
         nc.vector.scalar_tensor_tensor(
-            out=angle[:], in0=turns[:], scalar=-TWO_PI_HI, in1=phases, op0=ALU.mult, op1=ALU.add
+            out=angle[:], in0=turns[:], scalar=-TWO_PI_HI, in1=phases[:], op0=ALU.mult, op1=ALU.add
         )
         for piece in (TWO_PI_MID, TWO_PI_LO):
             nc.vector.scalar_tensor_tensor(
@@ -247,33 +256,13 @@ def tile_quantuminspiredneuralcore_pb_k_kernel(
         nc.vector.tensor_scalar(
             out=angle[:], in0=angle[:], scalar1=PI_BELOW, scalar2=-PI_BELOW, op0=ALU.min, op1=ALU.max
         )
-        sin_full = consts.tile([P, SLICES, 2], F32, name="sin_full")
-        nc.scalar.activation(out=sin_full[:], in_=angle[:], func=ACT.Sin)
-        sin_half = consts.tile([P, SLICES, 2], F32, name="sin_half")
-        nc.scalar.activation(out=sin_half[:], in_=angle[:], func=ACT.Sin, scale=0.5)
-        nc.scalar.activation(out=table_warm[:], in_=eps[:], func=ACT.Abs_reciprocal_sqrt)
-
-        half_sq = consts.tile([P, SLICES, 2], F32, name="half_sq")
-        nc.vector.tensor_tensor(out=half_sq[:], in0=sin_half[:], in1=sin_half[:], op=ALU.mult)
-        sin_less = consts.tile([P, SLICES, 2], F32, name="sin_less")
-        nc.vector.scalar_tensor_tensor(
-            out=sin_less[:], in0=half_sq[:], scalar=-2.0, in1=sin_full[:], op0=ALU.mult, op1=ALU.add
-        )
-        nc.vector.tensor_scalar(
-            out=cols[:, :, MOD : MOD + 2], in0=sin_less[:], scalar1=1.0, scalar2=None, op0=ALU.add
-        )
-        weighted_b = consts.tile([P, SLICES, 2], F32, name="weighted_b")
-        nc.vector.tensor_tensor(
-            out=weighted_b[:], in0=cols[:, :, PATH_B : PATH_B + 2], in1=cols[:, :, MOD : MOD + 2], op=ALU.mult
-        )
-        nc.vector.tensor_tensor(
-            out=cols[:, :, SHIFT : SHIFT + 1], in0=weighted_b[:, :, 0:1], in1=weighted_b[:, :, 1:2], op=ALU.add
-        )
+        sine = consts.tile([P, SLICES, 2], F32, name="sine")
+        nc.scalar.activation(out=sine[:], in_=angle[:], func=ACT.Sin)
 
         acc = [accs.tile([P, D], F32, name="acc%d" % i, tag="acc%d" % i) for i in range(TILES)]
 
         def planes_of(step):
-            return transpose_e(e_raw_of[step])
+            return transpose_e(*e_raw_of[step])
 
         e_planes = {0: planes_of(0)}
         e_grp_of = {}
@@ -302,6 +291,16 @@ def tile_quantuminspiredneuralcore_pb_k_kernel(
 
         for t in range(PATH_ROUND - AHEAD):
             stream_round(t)
+        nc.vector.tensor_scalar(
+            out=cols[:, :, MOD : MOD + 2], in0=sine[:], scalar1=SQRT_2, scalar2=None, op0=ALU.mult
+        )
+        weighted_b = consts.tile([P, SLICES, 2], F32, name="weighted_b")
+        nc.vector.tensor_tensor(
+            out=weighted_b[:], in0=cols[:, :, PATH_B : PATH_B + 2], in1=cols[:, :, MOD : MOD + 2], op=ALU.mult
+        )
+        nc.vector.tensor_tensor(
+            out=cols[:, :, SHIFT : SHIFT + 1], in0=weighted_b[:, :, 0:1], in1=weighted_b[:, :, 1:2], op=ALU.add
+        )
         path_raw = load_weight_rows(path_w.rearrange("w (p t) n -> p w t n", t=PACK))
         load_vectors((ENT_PB, ent_pb))
         h_sb = consts.tile([P, TILES, D], BF16, name="h_sb")
@@ -324,10 +323,7 @@ def tile_quantuminspiredneuralcore_pb_k_kernel(
         for t in range(STEPS, len(PIECES) + 1):
             stream_round(t)
         h_bias = [to_sbuf(h_bias_bank[i], "h_bias%d" % i) for i in range(TILES)]
-        ln3_g_row = to_sbuf(ln3_g_bank, "ln3_g_row")
-        ln3_b_row = to_sbuf(ln3_b_bank, "ln3_b_row")
-        ln4_g_row = to_sbuf(ln4_g_bank, "ln4_g_row")
-        ln4_b_row = to_sbuf(ln4_b_bank, "ln4_b_row")
+        nc.scalar.activation(out=table_warm[:], in_=eps[:], func=ACT.Abs_reciprocal_sqrt)
 
         def inverse_std(x, x_sum, label):
             squares = work.tile([P, D], F32, name="squares" + label)
@@ -409,12 +405,14 @@ def tile_quantuminspiredneuralcore_pb_k_kernel(
         both = range(TILES)
         x = [add_rows(acc[i][:], h_bias[i][:], "x%d" % i) for i in both]
         rstd = [inverse_std(x[i][0], x[i][1], "_a%d" % i) for i in both]
+        ln4_g_row = to_sbuf(ln4_g_bank, "ln4_g_row")
+        ln4_b_row = to_sbuf(ln4_b_bank, "ln4_b_row")
         neg_mean = [negative_mean(x[i][1], "_a%d" % i) for i in both]
-        centred = [centre(x[i][0], neg_mean[i], ln3_g_row, "_a%d" % i) for i in both]
-        hn_rounded = [scale_and_shift(centred[i], rstd[i], ln3_b_row, "hn_rounded%d" % i, BF16) for i in both]
+        centred = [centre(x[i][0], neg_mean[i], ln3_g_bank, "_a%d" % i) for i in both]
+        hn_rounded = [scale_and_shift(centred[i], rstd[i], ln3_b_bank, "hn_rounded%d" % i, BF16) for i in both]
         hn_bank = [transpose_hn(hn_rounded[i]) for i in both]
         hn_grp = [group_hn(i, hn_bank[i]) for i in both]
-        hn = [scale_and_shift(centred[i], rstd[i], ln3_b_row, "hn%d" % i) for i in both]
+        hn = [scale_and_shift(centred[i], rstd[i], ln3_b_bank, "hn%d" % i) for i in both]
         hn_codes = work.tile([P, TILES * P], U32, name="hn_codes", align_bytes=64)
         hn_scales = work.tile([P, TILES * P], U8, name="hn_scales", align_bytes=64)
         for i in both:

@@ -30,7 +30,7 @@ PIECES = (
 )
 AHEAD = 5
 E_LOADS = [(0, 1), (1, 1)] + [(s, 2) for s in range(2, STEPS, 2)]
-PATH_ROUND = 6
+PATH_ROUND = 7
 
 V_COLS = 288
 
@@ -185,10 +185,12 @@ def tile_quantuminspiredneuralcore_pb_k_kernel(
         def as_row(vector):
             return vector.rearrange("(o d) -> o d", o=1)
 
-        for row, vector in ((PHASE, phase), (PATH_B, path_b)):
-            nc.sync.dma_start(out=path_rows[row : row + vector.shape[0], :], in_=vector)
 
         w_raw_of = {}
+
+        def load_vectors(*rows):
+            for row, vector in rows:
+                nc.sync.dma_start(out=vec_rows[row : row + 1, :], in_=as_row(vector))
 
         def load_for_round(t):
             for first_step, steps in E_LOADS:
@@ -197,7 +199,10 @@ def tile_quantuminspiredneuralcore_pb_k_kernel(
             if t < len(PIECES):
                 w_raw_of[t] = load_w(t)
 
-        for t in range(AHEAD):
+        load_for_round(0)
+        for row, vector in ((PHASE, phase), (PATH_B, path_b)):
+            nc.sync.dma_start(out=path_rows[row : row + 2, :], in_=vector)
+        for t in range(1, AHEAD):
             load_for_round(t)
 
         ident_bf16 = consts.tile([P, P], BF16, name="ident_bf16")
@@ -207,14 +212,6 @@ def tile_quantuminspiredneuralcore_pb_k_kernel(
         nc.gpsimd.memset(vec_rows[:], 0.0)
         table_warm = consts.tile([P, 1], F32, name="table_warm")
         nc.scalar.activation(out=table_warm[:], in_=eps[:], func=ACT.Sin)
-
-        vec_bank = banks.tile([P, SLICES, P], BF16, name="vec_bank", tag="bank")
-        for s in range(SLICES):
-            nc.tensor.transpose(
-                out=vec_bank[:, s, :], in_=path_rows[:, s * P : (s + 1) * P], identity=ident_bf16[:]
-            )
-        cols = consts.tile([P, SLICES, COLUMNS], F32, name="cols")
-        nc.vector.tensor_copy(out=cols[:, :, PATH_B : PATH_B + 2], in_=vec_bank[:, :, PATH_B : PATH_B + 2])
 
         def spread_row(row, name, plus=None):
             bank = banks.tile([P, D], F32, name=name, tag="bank")
@@ -233,31 +230,6 @@ def tile_quantuminspiredneuralcore_pb_k_kernel(
             row = consts.tile([P, D], F32, name=name)
             nc.scalar.copy(out=row[:], in_=bank[:])
             return row
-
-        phases = consts.tile([P, SLICES, 2], F32, name="phases")
-        nc.vector.tensor_scalar(
-            out=phases[:], in0=vec_bank[:, :, PHASE : PHASE + 2], scalar1=QUARTER_PI, scalar2=None, op0=ALU.add
-        )
-        turns = consts.tile([P, SLICES, 2], F32, name="turns")
-        nc.vector.tensor_scalar(
-            out=turns[:], in0=phases[:], scalar1=INV_TWO_PI, scalar2=ROUND_MAGIC, op0=ALU.mult, op1=ALU.add
-        )
-        nc.vector.tensor_scalar(
-            out=turns[:], in0=turns[:], scalar1=ROUND_MAGIC, scalar2=None, op0=ALU.subtract
-        )
-        angle = consts.tile([P, SLICES, 2], F32, name="angle")
-        nc.vector.scalar_tensor_tensor(
-            out=angle[:], in0=turns[:], scalar=-TWO_PI_HI, in1=phases[:], op0=ALU.mult, op1=ALU.add
-        )
-        for piece in (TWO_PI_MID, TWO_PI_LO):
-            nc.vector.scalar_tensor_tensor(
-                out=angle[:], in0=turns[:], scalar=-piece, in1=angle[:], op0=ALU.mult, op1=ALU.add
-            )
-        nc.vector.tensor_scalar(
-            out=angle[:], in0=angle[:], scalar1=PI_BELOW, scalar2=-PI_BELOW, op0=ALU.min, op1=ALU.max
-        )
-        sine = consts.tile([P, SLICES, 2], F32, name="sine")
-        nc.scalar.activation(out=sine[:], in_=angle[:], func=ACT.Sin)
 
         acc = [accs.tile([P, D], F32, name="acc%d" % i, tag="acc%d" % i) for i in range(TILES)]
 
@@ -285,12 +257,49 @@ def tile_quantuminspiredneuralcore_pb_k_kernel(
             if t >= 1:
                 multiply(t - 1)
 
-        def load_vectors(*rows):
-            for row, vector in rows:
-                nc.sync.dma_start(out=vec_rows[row : row + 1, :], in_=as_row(vector))
+        stream_round(0)
 
-        for t in range(PATH_ROUND - AHEAD):
-            stream_round(t)
+        vec_bank = banks.tile([P, SLICES, P], BF16, name="vec_bank", tag="bank")
+        for s in range(SLICES):
+            nc.tensor.transpose(
+                out=vec_bank[:, s, :], in_=path_rows[:, s * P : (s + 1) * P], identity=ident_bf16[:]
+            )
+        cols = consts.tile([P, SLICES, COLUMNS], F32, name="cols")
+        nc.vector.tensor_copy(out=cols[:, :, PATH_B : PATH_B + 2], in_=vec_bank[:, :, PATH_B : PATH_B + 2])
+
+        phases = consts.tile([P, SLICES, 2], F32, name="phases")
+        nc.vector.tensor_scalar(
+            out=phases[:], in0=vec_bank[:, :, PHASE : PHASE + 2], scalar1=QUARTER_PI, scalar2=None, op0=ALU.add
+        )
+        turns = consts.tile([P, SLICES, 2], F32, name="turns")
+        nc.vector.tensor_scalar(
+            out=turns[:], in0=phases[:], scalar1=INV_TWO_PI, scalar2=ROUND_MAGIC, op0=ALU.mult, op1=ALU.add
+        )
+        nc.vector.tensor_scalar(
+            out=turns[:], in0=turns[:], scalar1=ROUND_MAGIC, scalar2=None, op0=ALU.subtract
+        )
+        angle = consts.tile([P, SLICES, 2], F32, name="angle")
+        nc.vector.scalar_tensor_tensor(
+            out=angle[:], in0=turns[:], scalar=-TWO_PI_HI, in1=phases[:], op0=ALU.mult, op1=ALU.add
+        )
+        for piece in (TWO_PI_MID, TWO_PI_LO):
+            nc.vector.scalar_tensor_tensor(
+                out=angle[:], in0=turns[:], scalar=-piece, in1=angle[:], op0=ALU.mult, op1=ALU.add
+            )
+        nc.vector.tensor_scalar(
+            out=angle[:], in0=angle[:], scalar1=PI_BELOW, scalar2=-PI_BELOW, op0=ALU.min, op1=ALU.max
+        )
+
+        stream_round(1)
+        sine = consts.tile([P, SLICES, 2], F32, name="sine")
+        nc.scalar.activation(out=sine[:], in_=angle[:], func=ACT.Sin)
+
+        path_raw = load_weight_rows(path_w.rearrange("w (p t) n -> p w t n", t=PACK))
+        load_vectors((ENT_PB, ent_pb))
+        h_sb = consts.tile([P, TILES, D], BF16, name="h_sb")
+        nc.sync.dma_start(out=h_sb[:], in_=h.rearrange("b s d -> s b d"))
+
+        stream_round(2)
         nc.vector.tensor_scalar(
             out=cols[:, :, MOD : MOD + 2], in0=sine[:], scalar1=SQRT_2, scalar2=None, op0=ALU.mult
         )
@@ -301,11 +310,7 @@ def tile_quantuminspiredneuralcore_pb_k_kernel(
         nc.vector.tensor_tensor(
             out=cols[:, :, SHIFT : SHIFT + 1], in0=weighted_b[:, :, 0:1], in1=weighted_b[:, :, 1:2], op=ALU.add
         )
-        path_raw = load_weight_rows(path_w.rearrange("w (p t) n -> p w t n", t=PACK))
-        load_vectors((ENT_PB, ent_pb))
-        h_sb = consts.tile([P, TILES, D], BF16, name="h_sb")
-        nc.sync.dma_start(out=h_sb[:], in_=h.rearrange("b s d -> s b d"))
-        for t in range(PATH_ROUND - AHEAD, PATH_ROUND):
+        for t in range(3, PATH_ROUND):
             stream_round(t)
         path_grp = regroup_weights(path_raw)
         stream_round(PATH_ROUND)

@@ -36,10 +36,10 @@ V_COLS = 288
 
 FLOPS = 2 * TILES * P * K * D + 2 * 2 * TILES * P * D * D
 
-PATH_B, PHASE = 0, 2
-MOD = 2
-SHIFT = 4
-COLUMNS = 5
+PATH_B, LN3_B_COLUMN, PHASE = 0, 2, 3
+MOD = 3
+SHIFT = 5
+COLUMNS = 6
 ENT_PB, LN3_G, LN3_B, LN4_G, LN4_B = range(5)
 
 TWO_PI_HI = 6.28125
@@ -200,8 +200,8 @@ def tile_quantuminspiredneuralcore_pb_k_kernel(
                 w_raw_of[t] = load_w(t)
 
         load_for_round(0)
-        for row, vector in ((PHASE, phase), (PATH_B, path_b)):
-            nc.sync.dma_start(out=path_rows[row : row + 2, :], in_=vector)
+        for row, vector in ((PHASE, phase), (PATH_B, path_b), (LN3_B_COLUMN, as_row(ln3_b))):
+            nc.sync.dma_start(out=path_rows[row : row + vector.shape[0], :], in_=vector)
         for t in range(1, AHEAD):
             load_for_round(t)
 
@@ -265,7 +265,7 @@ def tile_quantuminspiredneuralcore_pb_k_kernel(
                 out=vec_bank[:, s, :], in_=path_rows[:, s * P : (s + 1) * P], identity=ident_bf16[:]
             )
         cols = consts.tile([P, SLICES, COLUMNS], F32, name="cols")
-        nc.vector.tensor_copy(out=cols[:, :, PATH_B : PATH_B + 2], in_=vec_bank[:, :, PATH_B : PATH_B + 2])
+        nc.vector.tensor_copy(out=cols[:, :, 0:MOD], in_=vec_bank[:, :, 0:MOD])
 
         phases = consts.tile([P, SLICES, 2], F32, name="phases")
         nc.vector.tensor_scalar(
@@ -310,6 +310,12 @@ def tile_quantuminspiredneuralcore_pb_k_kernel(
         nc.vector.tensor_tensor(
             out=cols[:, :, SHIFT : SHIFT + 1], in0=weighted_b[:, :, 0:1], in1=weighted_b[:, :, 1:2], op=ALU.add
         )
+        nc.vector.tensor_tensor(
+            out=cols[:, :, SHIFT : SHIFT + 1],
+            in0=cols[:, :, SHIFT : SHIFT + 1],
+            in1=cols[:, :, LN3_B_COLUMN : LN3_B_COLUMN + 1],
+            op=ALU.add,
+        )
         for t in range(3, PATH_ROUND):
             stream_round(t)
         path_grp = regroup_weights(path_raw)
@@ -328,6 +334,8 @@ def tile_quantuminspiredneuralcore_pb_k_kernel(
         for t in range(STEPS, len(PIECES) + 1):
             stream_round(t)
         h_bias = [to_sbuf(h_bias_bank[i], "h_bias%d" % i) for i in range(TILES)]
+        ln4_g_row = to_sbuf(ln4_g_bank, "ln4_g_row")
+        ln4_b_row = to_sbuf(ln4_b_bank, "ln4_b_row")
         nc.scalar.activation(out=table_warm[:], in_=eps[:], func=ACT.Abs_reciprocal_sqrt)
 
         def inverse_std(x, x_sum, label):
@@ -363,22 +371,24 @@ def tile_quantuminspiredneuralcore_pb_k_kernel(
             )
             return result
 
-        def add_rows(in0, in1, name):
+        def add_rows(in0, scale, in1, name):
             total = work.tile([P, D], F32, name=name)
             total_sum = small.tile([P, 1], F32, name=name + "_sum")
             nc.vector.scalar_tensor_tensor(
-                out=total[:], in0=in0, scalar=1.0, in1=in1, op0=ALU.mult, op1=ALU.add, accum_out=total_sum[:]
+                out=total[:], in0=in0, scalar=scale, in1=in1, op0=ALU.mult, op1=ALU.add, accum_out=total_sum[:]
             )
             return total, total_sum
 
-        def transpose_hn(hn_rounded):
+        def keep_clock_up(bank, count):
+            for n in range(count):
+                nc.tensor.matmul(out=bank[:], lhsT=ident_bf16[:], rhs=vec_rows[:], start=True, stop=True)
+
+        def transpose_hn(hn_rounded, hn_bank):
             words = hn_rounded[:].bitcast(F32)
-            hn_bank = banks.tile([P, 2, P], F32, name="hn_bank", tag="bank")
             for u in range(2):
                 nc.tensor.transpose(
                     out=hn_bank[:, u, :], in_=words[:, u : D // 2 : 2], identity=ident_f32[:]
                 )
-            return hn_bank
 
         def group_hn(i, hn_bank):
             hn_grp = work.tile([P, P * 2], F32, name="hn_grp%d" % i, align_bytes=64)
@@ -388,72 +398,79 @@ def tile_quantuminspiredneuralcore_pb_k_kernel(
             return hn_grp
 
         def quantise_hn(i, hn_grp):
-            nc.vector.quantize_mx(
-                out=hn_codes[:, i * P : (i + 1) * P].bitcast(FP8X4),
-                scales=hn_scales[:, i * P : (i + 1) * P],
-                in_=hn_grp[:].bitcast(BF16),
-            )
+            codes = work.tile([P, P], U32, name="hn_codes%d" % i, align_bytes=64)
+            scales = work.tile([P, P], U8, name="hn_scales%d" % i, align_bytes=64)
+            nc.vector.quantize_mx(out=codes[:].bitcast(FP8X4), scales=scales[:], in_=hn_grp[:].bitcast(BF16))
+            return codes, scales
 
-        def pathway(w, f, out):
+        def pathways(hn_op):
             path_codes, path_scales = path_op
-            first = w * D + f * P
-            nc.tensor.matmul_mx(
-                out=out,
-                lhsT=path_codes[:, first : first + P].bitcast(FP8X4),
-                lhsT_scale=path_scales[:, first : first + P],
-                rhs=hn_codes[:].bitcast(FP8X4),
-                rhs_scale=hn_scales[:],
-                start=True,
-                stop=True,
-            )
+            hn_codes, hn_scales = hn_op
+            products = []
+            for w in range(2):
+                product = banks.tile([P, SLICES, P], F32, name="product", tag="bank")
+                for f in range(SLICES):
+                    first = w * D + f * P
+                    nc.tensor.matmul_mx(
+                        out=product[:, f, :],
+                        lhsT=path_codes[:, first : first + P].bitcast(FP8X4),
+                        lhsT_scale=path_scales[:, first : first + P],
+                        rhs=hn_codes[:].bitcast(FP8X4),
+                        rhs_scale=hn_scales[:],
+                        start=True,
+                        stop=True,
+                    )
+                products.append(product)
+            return products
+
+        def interfere(i, products):
+            first_term = work.tile([P, SLICES, P], F32, name="first_term%d" % i)
+            interf = work.tile([P, SLICES, P], F32, name="interf%d" % i)
+            for f in range(SLICES):
+                nc.scalar.activation(
+                    out=first_term[:, f, :],
+                    in_=products[0][:, f, :],
+                    func=ACT.Identity,
+                    scale=cols[:, f, MOD : MOD + 1],
+                    bias=cols[:, f, SHIFT : SHIFT + 1],
+                )
+                nc.vector.scalar_tensor_tensor(
+                    out=interf[:, f, :],
+                    in0=products[1][:, f, :],
+                    scalar=cols[:, f, MOD + 1 : MOD + 2],
+                    in1=first_term[:, f, :],
+                    op0=ALU.mult,
+                    op1=ALU.add,
+                )
+            return interf
+
+        def transpose_back(i, interf):
+            bank = accs.tile([P, D], F32, name="interf_bank%d" % i, tag="acc%d" % i)
+            for f in range(SLICES):
+                nc.tensor.transpose(
+                    out=bank[:, f * P : (f + 1) * P], in_=interf[:, f, :], identity=ident_f32[:]
+                )
+            return bank
 
         both = range(TILES)
-        x = [add_rows(acc[i][:], h_bias[i][:], "x%d" % i) for i in both]
+        x = [add_rows(acc[i][:], 1.0, h_bias[i][:], "x%d" % i) for i in both]
         rstd = [inverse_std(x[i][0], x[i][1], "_a%d" % i) for i in both]
-        ln4_g_row = to_sbuf(ln4_g_bank, "ln4_g_row")
-        ln4_b_row = to_sbuf(ln4_b_bank, "ln4_b_row")
         neg_mean = [negative_mean(x[i][1], "_a%d" % i) for i in both]
         centred = [centre(x[i][0], neg_mean[i], ln3_g_bank, "_a%d" % i) for i in both]
         hn_rounded = [scale_and_shift(centred[i], rstd[i], ln3_b_bank, "hn_rounded%d" % i, BF16) for i in both]
-        hn_bank = [transpose_hn(hn_rounded[i]) for i in both]
+        keep_clock_up(accs.tile([P, D], F32, name="idle_bank", tag="acc0"), 5)
+        hn_bank = [banks.tile([P, 2, P], F32, name="hn_bank", tag="bank") for i in both]
+        idle_bank = banks.tile([P, D], F32, name="idle_bank2", tag="bank")
+        keep_clock_up(idle_bank, 3)
+        for i in both:
+            transpose_hn(hn_rounded[i], hn_bank[i])
+        keep_clock_up(idle_bank, 1)
         hn_grp = [group_hn(i, hn_bank[i]) for i in both]
-        hn = [scale_and_shift(centred[i], rstd[i], ln3_b_bank, "hn%d" % i) for i in both]
-        hn_codes = work.tile([P, TILES * P], U32, name="hn_codes", align_bytes=64)
-        hn_scales = work.tile([P, TILES * P], U8, name="hn_scales", align_bytes=64)
-        for i in both:
-            quantise_hn(i, hn_grp[i])
-
-        tokens = TILES * P
-        interf = work.tile([P, SLICES, tokens], F32, name="interf")
-        first_term = work.tile([P, SLICES, tokens], F32, name="first_term")
-        for f in range(SLICES):
-            product = [banks.tile([P, tokens], F32, name="product", tag="bank") for w in range(2)]
-            for w in range(2):
-                pathway(w, f, product[w][:])
-            nc.scalar.activation(
-                out=first_term[:, f, :],
-                in_=product[0][:],
-                func=ACT.Identity,
-                scale=cols[:, f, MOD : MOD + 1],
-                bias=cols[:, f, SHIFT : SHIFT + 1],
-            )
-            nc.vector.scalar_tensor_tensor(
-                out=interf[:, f, :],
-                in0=product[1][:],
-                scalar=cols[:, f, MOD + 1 : MOD + 2],
-                in1=first_term[:, f, :],
-                op0=ALU.mult,
-                op1=ALU.add,
-            )
-        interf_bank = [accs.tile([P, D], F32, name="interf_bank%d" % i, tag="acc%d" % i) for i in both]
-        for i in both:
-            for f in range(SLICES):
-                nc.tensor.transpose(
-                    out=interf_bank[i][:, f * P : (f + 1) * P],
-                    in_=interf[:, f, i * P : (i + 1) * P],
-                    identity=ident_f32[:],
-                )
-        y = [add_rows(interf_bank[i][:], hn[i][:], "y%d" % i) for i in both]
+        hn_op = [quantise_hn(i, hn_grp[i]) for i in both]
+        products = [pathways(hn_op[i]) for i in both]
+        interf = [interfere(i, products[i]) for i in both]
+        interf_bank = [transpose_back(i, interf[i]) for i in both]
+        y = [add_rows(centred[i][:], rstd[i][:, 0:1], interf_bank[i][:], "y%d" % i) for i in both]
         rstd = [inverse_std(y[i][0], y[i][1], "_b%d" % i) for i in both]
         neg_mean = [negative_mean(y[i][1], "_b%d" % i) for i in both]
         centred = [centre(y[i][0], neg_mean[i], ln4_g_row, "_b%d" % i) for i in both]

@@ -30,9 +30,11 @@ PIECES = (
 )
 AHEAD = 5
 E_LOADS = [(0, 1), (1, 1)] + [(s, 2) for s in range(2, STEPS, 2)]
-PATH_ROUND = 7
+SMALL_ROUND = 3
+LATE_ROUND = 7
 
-V_COLS = 288
+V_COLS = 296
+V_PATH_COLS = 192
 
 FLOPS = 2 * TILES * P * K * D + 2 * 2 * TILES * P * D * D
 
@@ -66,7 +68,8 @@ def tile_quantuminspiredneuralcore_pb_k_kernel(
         work = ctx.enter_context(tc.tile_pool(name="work", bufs=1))
         small = ctx.enter_context(tc.tile_pool(name="small", bufs=1))
         accs = ctx.enter_context(tc.psum_pool(name="accs", bufs=1))
-        banks = ctx.enter_context(tc.psum_pool(name="banks", bufs=6))
+        banks = ctx.enter_context(tc.psum_pool(name="banks", bufs=4))
+        row_banks = ctx.enter_context(tc.psum_pool(name="row_banks", bufs=2))
 
         def load_weight_rows(view):
             w_raw = w_raws.tile(list(view.shape), BF16, name="w_raw", tag="w_raw")
@@ -90,28 +93,37 @@ def tile_quantuminspiredneuralcore_pb_k_kernel(
             for s in range(steps):
                 e_raw_of[first_step + s] = (e_raw, s)
 
-        def regroup_weights(w_raw):
-            passes = w_raw.shape[1]
-            w_grp = grouped.tile([P, passes, D, PACK], BF16, name="w_grp", tag="w_grp", align_bytes=64)
+        def grouped_tile(w_raw):
+            return grouped.tile([P, w_raw.shape[1], D, PACK], BF16, name="w_grp", tag="w_grp", align_bytes=64)
+
+        def regroup_on_vector(w_raw, w_grp, columns):
             nc.vector.tensor_copy(
-                out=w_grp[:, :, 0:V_COLS, :].rearrange("p c (a i) t -> p c a t i", i=4),
-                in_=w_raw[:, :, :, 0:V_COLS].rearrange("p c t (a i) -> p c a t i", i=4),
+                out=w_grp[:, :, 0:columns, :].rearrange("p c (a i) t -> p c a t i", i=4),
+                in_=w_raw[:, :, :, 0:columns].rearrange("p c t (a i) -> p c a t i", i=4),
             )
-            for c in range(passes):
-                nc.scalar.copy(
-                    out=w_grp[:, c, V_COLS:D, :].rearrange("p (a i) t -> p a t i", i=4),
-                    in_=w_raw[:, c, :, V_COLS:D].rearrange("p t (a i) -> p a t i", i=4),
-                )
+
+        def regroup_on_scalar(w_raw, w_grp, c, columns):
+            nc.scalar.copy(
+                out=w_grp[:, c, columns:D, :].rearrange("p (a i) t -> p a t i", i=4),
+                in_=w_raw[:, c, :, columns:D].rearrange("p t (a i) -> p a t i", i=4),
+            )
+
+        def regroup_weights(w_raw):
+            w_grp = grouped_tile(w_raw)
+            regroup_on_vector(w_raw, w_grp, V_COLS)
+            for c in range(w_raw.shape[1]):
+                regroup_on_scalar(w_raw, w_grp, c, V_COLS)
             return w_grp
 
-        def quantise_weights(w_grp, pool):
-            passes = w_grp.shape[1]
-            codes = pool.tile([P, passes * D], U32, name="w_codes", tag="w_codes", align_bytes=64)
-            scales = pool.tile([P, passes * D], U8, name="w_scales", tag="w_scales", align_bytes=64)
+        def quantise_weights(w_grp, first, passes, pool, label=""):
+            name = "w_codes" + label
+            codes = pool.tile([P, passes * D], U32, name=name, tag=name, align_bytes=64)
+            name = "w_scales" + label
+            scales = pool.tile([P, passes * D], U8, name=name, tag=name, align_bytes=64)
             nc.vector.quantize_mx(
                 out=codes[:].bitcast(FP8X4),
                 scales=scales[:],
-                in_=w_grp[:].rearrange("p c n t -> p (c n t)"),
+                in_=w_grp[:, first : first + passes].rearrange("p c n t -> p (c n t)"),
             )
             return codes, scales
 
@@ -185,8 +197,8 @@ def tile_quantuminspiredneuralcore_pb_k_kernel(
         def as_row(vector):
             return vector.rearrange("(o d) -> o d", o=1)
 
-
         w_raw_of = {}
+        path_raw_of = {}
 
         def load_vectors(*rows):
             for row, vector in rows:
@@ -194,15 +206,18 @@ def tile_quantuminspiredneuralcore_pb_k_kernel(
 
         def load_for_round(t):
             for first_step, steps in E_LOADS:
-                if first_step == t:
+                if first_step == t - 1:
                     load_e(first_step, steps)
             if t < len(PIECES):
                 w_raw_of[t] = load_w(t)
+            if t == len(PIECES):
+                path_raw_of[0] = load_weight_rows(path_w.rearrange("w (p t) n -> p w t n", t=PACK))
 
-        load_for_round(0)
+        for t in range(3):
+            load_for_round(t)
         for row, vector in ((PHASE, phase), (PATH_B, path_b), (LN3_B_COLUMN, as_row(ln3_b))):
             nc.sync.dma_start(out=path_rows[row : row + vector.shape[0], :], in_=vector)
-        for t in range(1, AHEAD):
+        for t in range(3, AHEAD):
             load_for_round(t)
 
         ident_bf16 = consts.tile([P, P], BF16, name="ident_bf16")
@@ -213,8 +228,8 @@ def tile_quantuminspiredneuralcore_pb_k_kernel(
         table_warm = consts.tile([P, 1], F32, name="table_warm")
         nc.scalar.activation(out=table_warm[:], in_=eps[:], func=ACT.Sin)
 
-        def spread_row(row, name, plus=None):
-            bank = banks.tile([P, D], F32, name=name, tag="bank")
+        def spread_row(row, pool, name, plus=None):
+            bank = pool.tile([P, D], F32, name=name, tag="bank")
             if plus is not None:
                 nc.tensor.matmul(out=bank[:], lhsT=ident_bf16[:], rhs=plus, start=True, stop=False)
             nc.tensor.matmul(
@@ -236,7 +251,54 @@ def tile_quantuminspiredneuralcore_pb_k_kernel(
         def planes_of(step):
             return transpose_e(*e_raw_of[step])
 
-        e_planes = {0: planes_of(0)}
+        cols = consts.tile([P, SLICES, COLUMNS], F32, name="cols")
+        phases = consts.tile([P, SLICES, 2], F32, name="phases")
+        turns = consts.tile([P, SLICES, 2], F32, name="turns")
+        angle = consts.tile([P, SLICES, 2], F32, name="angle")
+        sine = consts.tile([P, SLICES, 2], F32, name="sine")
+        weighted_b = consts.tile([P, SLICES, 2], F32, name="weighted_b")
+        mods = cols[:, :, MOD : MOD + 2]
+        shift = cols[:, :, SHIFT : SHIFT + 1]
+
+        def add_turns(of_a_turn, to):
+            nc.vector.scalar_tensor_tensor(
+                out=angle[:], in0=turns[:], scalar=-of_a_turn, in1=to, op0=ALU.mult, op1=ALU.add
+            )
+
+        def scalars(out, in0, scalar1, op0, scalar2=None, op1=None):
+            if op1 is None:
+                nc.vector.tensor_scalar(out=out, in0=in0, scalar1=scalar1, scalar2=None, op0=op0)
+            else:
+                nc.vector.tensor_scalar(out=out, in0=in0, scalar1=scalar1, scalar2=scalar2, op0=op0, op1=op1)
+
+        small_steps = [
+            lambda: nc.vector.tensor_copy(out=cols[:, :, 0:MOD], in_=vec_bank[:, :, 0:MOD]),
+            lambda: scalars(phases[:], vec_bank[:, :, PHASE : PHASE + 2], QUARTER_PI, ALU.add),
+            lambda: scalars(turns[:], phases[:], INV_TWO_PI, ALU.mult, ROUND_MAGIC, ALU.add),
+            lambda: scalars(turns[:], turns[:], ROUND_MAGIC, ALU.subtract),
+            lambda: add_turns(TWO_PI_HI, phases[:]),
+            lambda: add_turns(TWO_PI_MID, angle[:]),
+            lambda: add_turns(TWO_PI_LO, angle[:]),
+            lambda: scalars(angle[:], angle[:], PI_BELOW, ALU.min, -PI_BELOW, ALU.max),
+            lambda: nc.scalar.activation(out=sine[:], in_=angle[:], func=ACT.Sin),
+            lambda: scalars(mods, sine[:], SQRT_2, ALU.mult),
+            lambda: nc.vector.tensor_tensor(
+                out=weighted_b[:], in0=cols[:, :, PATH_B : PATH_B + 2], in1=mods, op=ALU.mult
+            ),
+            lambda: nc.vector.tensor_tensor(
+                out=shift, in0=weighted_b[:, :, 0:1], in1=weighted_b[:, :, 1:2], op=ALU.add
+            ),
+            lambda: nc.vector.tensor_tensor(
+                out=shift, in0=shift, in1=cols[:, :, LN3_B_COLUMN : LN3_B_COLUMN + 1], op=ALU.add
+            ),
+        ]
+
+        def small_step(t, place):
+            step = 3 * (t - SMALL_ROUND) + place
+            if 0 <= step < len(small_steps):
+                small_steps[step]()
+
+        e_planes = {}
         e_grp_of = {}
         e_op = {}
         w_grp_of = {}
@@ -244,98 +306,52 @@ def tile_quantuminspiredneuralcore_pb_k_kernel(
 
         def stream_round(t):
             load_for_round(t + AHEAD)
-            if t + 1 < STEPS:
-                e_planes[t + 1] = planes_of(t + 1)
             if t < STEPS:
-                e_grp_of[t] = copy_e(e_planes[t])
+                e_planes[t] = transpose_e(*e_raw_of[t])
             if 1 <= t <= STEPS:
-                e_op[t - 1] = quantise_e(e_grp_of[t - 1])
+                e_grp_of[t - 1] = copy_e(e_planes[t - 1])
+            if 2 <= t <= STEPS + 1:
+                e_op[t - 2] = quantise_e(e_grp_of[t - 2])
+            small_step(t, 0)
             if t >= 1:
-                w_op[t - 1] = quantise_weights(w_grp_of[t - 1], w_quant)
+                w_op[t - 1] = quantise_weights(w_grp_of[t - 1], 0, PIECES[t - 1][1], w_quant)
+            small_step(t, 1)
             if t < len(PIECES):
                 w_grp_of[t] = regroup_weights(w_raw_of[t])
-            if t >= 1:
+            small_step(t, 2)
+            if t == 2:
+                multiply(0)
+            if t >= 2:
                 multiply(t - 1)
 
         stream_round(0)
-
-        vec_bank = banks.tile([P, SLICES, P], BF16, name="vec_bank", tag="bank")
+        load_vectors((ENT_PB, ent_pb))
+        h_sb = consts.tile([P, TILES, D], BF16, name="h_sb")
+        nc.sync.dma_start(out=h_sb[:], in_=h.rearrange("b s d -> s b d"))
+        stream_round(1)
+        vec_bank = row_banks.tile([P, SLICES, P], BF16, name="vec_bank", tag="bank")
         for s in range(SLICES):
             nc.tensor.transpose(
                 out=vec_bank[:, s, :], in_=path_rows[:, s * P : (s + 1) * P], identity=ident_bf16[:]
             )
-        cols = consts.tile([P, SLICES, COLUMNS], F32, name="cols")
-        nc.vector.tensor_copy(out=cols[:, :, 0:MOD], in_=vec_bank[:, :, 0:MOD])
-
-        phases = consts.tile([P, SLICES, 2], F32, name="phases")
-        nc.vector.tensor_scalar(
-            out=phases[:], in0=vec_bank[:, :, PHASE : PHASE + 2], scalar1=QUARTER_PI, scalar2=None, op0=ALU.add
-        )
-        turns = consts.tile([P, SLICES, 2], F32, name="turns")
-        nc.vector.tensor_scalar(
-            out=turns[:], in0=phases[:], scalar1=INV_TWO_PI, scalar2=ROUND_MAGIC, op0=ALU.mult, op1=ALU.add
-        )
-        nc.vector.tensor_scalar(
-            out=turns[:], in0=turns[:], scalar1=ROUND_MAGIC, scalar2=None, op0=ALU.subtract
-        )
-        angle = consts.tile([P, SLICES, 2], F32, name="angle")
-        nc.vector.scalar_tensor_tensor(
-            out=angle[:], in0=turns[:], scalar=-TWO_PI_HI, in1=phases[:], op0=ALU.mult, op1=ALU.add
-        )
-        for piece in (TWO_PI_MID, TWO_PI_LO):
-            nc.vector.scalar_tensor_tensor(
-                out=angle[:], in0=turns[:], scalar=-piece, in1=angle[:], op0=ALU.mult, op1=ALU.add
-            )
-        nc.vector.tensor_scalar(
-            out=angle[:], in0=angle[:], scalar1=PI_BELOW, scalar2=-PI_BELOW, op0=ALU.min, op1=ALU.max
-        )
-
-        stream_round(1)
-        sine = consts.tile([P, SLICES, 2], F32, name="sine")
-        nc.scalar.activation(out=sine[:], in_=angle[:], func=ACT.Sin)
-
-        path_raw = load_weight_rows(path_w.rearrange("w (p t) n -> p w t n", t=PACK))
-        load_vectors((ENT_PB, ent_pb))
-        h_sb = consts.tile([P, TILES, D], BF16, name="h_sb")
-        nc.sync.dma_start(out=h_sb[:], in_=h.rearrange("b s d -> s b d"))
-
-        stream_round(2)
-        nc.vector.tensor_scalar(
-            out=cols[:, :, MOD : MOD + 2], in0=sine[:], scalar1=SQRT_2, scalar2=None, op0=ALU.mult
-        )
-        weighted_b = consts.tile([P, SLICES, 2], F32, name="weighted_b")
-        nc.vector.tensor_tensor(
-            out=weighted_b[:], in0=cols[:, :, PATH_B : PATH_B + 2], in1=cols[:, :, MOD : MOD + 2], op=ALU.mult
-        )
-        nc.vector.tensor_tensor(
-            out=cols[:, :, SHIFT : SHIFT + 1], in0=weighted_b[:, :, 0:1], in1=weighted_b[:, :, 1:2], op=ALU.add
-        )
-        nc.vector.tensor_tensor(
-            out=cols[:, :, SHIFT : SHIFT + 1],
-            in0=cols[:, :, SHIFT : SHIFT + 1],
-            in1=cols[:, :, LN3_B_COLUMN : LN3_B_COLUMN + 1],
-            op=ALU.add,
-        )
-        for t in range(3, PATH_ROUND):
+        for t in range(2, LATE_ROUND):
             stream_round(t)
-        path_grp = regroup_weights(path_raw)
-        stream_round(PATH_ROUND)
-        path_op = quantise_weights(path_grp, consts)
-        load_vectors((LN3_G, ln3_g), (LN3_B, ln3_b))
-        stream_round(PATH_ROUND + 1)
-        load_vectors((LN4_G, ln4_g), (LN4_B, ln4_b))
-        for t in range(PATH_ROUND + 2, STEPS):
+        load_vectors((LN3_G, ln3_g), (LN3_B, ln3_b), (LN4_G, ln4_g), (LN4_B, ln4_b))
+        for t in range(LATE_ROUND, STEPS):
             stream_round(t)
-        h_bias_bank = [spread_row(ENT_PB, "h_bias_bank%d" % i, plus=h_sb[:, i, :]) for i in range(TILES)]
-        ln3_g_bank = spread_row(LN3_G, "ln3_g_bank")
-        ln3_b_bank = spread_row(LN3_B, "ln3_b_bank")
-        ln4_g_bank = spread_row(LN4_G, "ln4_g_bank")
-        ln4_b_bank = spread_row(LN4_B, "ln4_b_bank")
-        for t in range(STEPS, len(PIECES) + 1):
+        h_bias_bank = [spread_row(ENT_PB, banks, "h_bias_bank%d" % i, plus=h_sb[:, i, :]) for i in range(TILES)]
+        ln4_g_bank = spread_row(LN4_G, row_banks, "ln4_g_bank")
+        ln4_b_bank = spread_row(LN4_B, row_banks, "ln4_b_bank")
+        stream_round(STEPS)
+        ln3_g_bank = spread_row(LN3_G, banks, "ln3_g_bank")
+        ln3_b_bank = spread_row(LN3_B, banks, "ln3_b_bank")
+        for t in range(STEPS + 1, len(PIECES) + 1):
             stream_round(t)
         h_bias = [to_sbuf(h_bias_bank[i], "h_bias%d" % i) for i in range(TILES)]
-        ln4_g_row = to_sbuf(ln4_g_bank, "ln4_g_row")
-        ln4_b_row = to_sbuf(ln4_b_bank, "ln4_b_row")
+        path_raw = path_raw_of[0]
+        path_grp = grouped_tile(path_raw)
+        regroup_on_vector(path_raw, path_grp, V_PATH_COLS)
+        regroup_on_scalar(path_raw, path_grp, 0, V_PATH_COLS)
         nc.scalar.activation(out=table_warm[:], in_=eps[:], func=ACT.Abs_reciprocal_sqrt)
 
         def inverse_std(x, x_sum, label):
@@ -383,12 +399,14 @@ def tile_quantuminspiredneuralcore_pb_k_kernel(
             for n in range(count):
                 nc.tensor.matmul(out=bank[:], lhsT=ident_bf16[:], rhs=vec_rows[:], start=True, stop=True)
 
-        def transpose_hn(hn_rounded, hn_bank):
+        def transpose_hn(hn_rounded):
             words = hn_rounded[:].bitcast(F32)
+            hn_bank = banks.tile([P, 2, P], F32, name="hn_bank", tag="bank")
             for u in range(2):
                 nc.tensor.transpose(
                     out=hn_bank[:, u, :], in_=words[:, u : D // 2 : 2], identity=ident_f32[:]
                 )
+            return hn_bank
 
         def group_hn(i, hn_bank):
             hn_grp = work.tile([P, P * 2], F32, name="hn_grp%d" % i, align_bytes=64)
@@ -404,13 +422,13 @@ def tile_quantuminspiredneuralcore_pb_k_kernel(
             return codes, scales
 
         def pathways(hn_op):
-            path_codes, path_scales = path_op
             hn_codes, hn_scales = hn_op
             products = []
             for w in range(2):
+                path_codes, path_scales = path_op[w]
                 product = banks.tile([P, SLICES, P], F32, name="product", tag="bank")
                 for f in range(SLICES):
-                    first = w * D + f * P
+                    first = f * P
                     nc.tensor.matmul_mx(
                         out=product[:, f, :],
                         lhsT=path_codes[:, first : first + P].bitcast(FP8X4),
@@ -455,25 +473,38 @@ def tile_quantuminspiredneuralcore_pb_k_kernel(
         both = range(TILES)
         x = [add_rows(acc[i][:], 1.0, h_bias[i][:], "x%d" % i) for i in both]
         rstd = [inverse_std(x[i][0], x[i][1], "_a%d" % i) for i in both]
+        regroup_on_scalar(path_raw, path_grp, 1, V_PATH_COLS)
         neg_mean = [negative_mean(x[i][1], "_a%d" % i) for i in both]
         centred = [centre(x[i][0], neg_mean[i], ln3_g_bank, "_a%d" % i) for i in both]
         hn_rounded = [scale_and_shift(centred[i], rstd[i], ln3_b_bank, "hn_rounded%d" % i, BF16) for i in both]
-        keep_clock_up(accs.tile([P, D], F32, name="idle_bank", tag="acc0"), 5)
-        hn_bank = [banks.tile([P, 2, P], F32, name="hn_bank", tag="bank") for i in both]
-        idle_bank = banks.tile([P, D], F32, name="idle_bank2", tag="bank")
-        keep_clock_up(idle_bank, 3)
-        for i in both:
-            transpose_hn(hn_rounded[i], hn_bank[i])
+        idle_bank = accs.tile([P, D], F32, name="idle_bank", tag="acc1")
+        keep_clock_up(idle_bank, 7)
+        hn_bank = [transpose_hn(hn_rounded[i]) for i in both]
         keep_clock_up(idle_bank, 1)
         hn_grp = [group_hn(i, hn_bank[i]) for i in both]
-        hn_op = [quantise_hn(i, hn_grp[i]) for i in both]
+        path_op = []
+        hn_op = []
+        for i in both:
+            path_op.append(quantise_weights(path_grp, i, 1, consts, "_path%d" % i))
+            hn_op.append(quantise_hn(i, hn_grp[i]))
         products = [pathways(hn_op[i]) for i in both]
         interf = [interfere(i, products[i]) for i in both]
         interf_bank = [transpose_back(i, interf[i]) for i in both]
         y = [add_rows(centred[i][:], rstd[i][:, 0:1], interf_bank[i][:], "y%d" % i) for i in both]
         rstd = [inverse_std(y[i][0], y[i][1], "_b%d" % i) for i in both]
         neg_mean = [negative_mean(y[i][1], "_b%d" % i) for i in both]
-        centred = [centre(y[i][0], neg_mean[i], ln4_g_row, "_b%d" % i) for i in both]
+        centred = [centre(y[i][0], neg_mean[i], ln4_g_bank, "_b%d" % i) for i in both]
         for i in both:
-            result = scale_and_shift(centred[i], rstd[i], ln4_b_row, "result%d" % i)
-            nc.sync.dma_start(out=out[i], in_=result[:])
+            result = work.tile([P, D], F32, name="result%d" % i)
+            width = D if i < TILES - 1 else D // 2
+            for first in range(0, D, width):
+                part = slice(first, first + width)
+                nc.vector.scalar_tensor_tensor(
+                    out=result[:, part],
+                    in0=centred[i][:, part],
+                    scalar=rstd[i][:, 0:1],
+                    in1=ln4_b_bank[:, part],
+                    op0=ALU.mult,
+                    op1=ALU.add,
+                )
+                nc.sync.dma_start(out=out[i, :, part], in_=result[:, part])

@@ -31,10 +31,9 @@ PIECES = (
 AHEAD = 5
 E_LOADS = [(0, 1), (1, 1)] + [(s, 2) for s in range(2, STEPS, 2)]
 SMALL_ROUND = 3
-LATE_ROUND = 7
+PATH_ROUND = 6
 
-V_COLS = 296
-V_PATH_COLS = 192
+V_COLS = 288
 
 FLOPS = 2 * TILES * P * K * D + 2 * 2 * TILES * P * D * D
 
@@ -198,7 +197,6 @@ def tile_quantuminspiredneuralcore_pb_k_kernel(
             return vector.rearrange("(o d) -> o d", o=1)
 
         w_raw_of = {}
-        path_raw_of = {}
 
         def load_vectors(*rows):
             for row, vector in rows:
@@ -210,8 +208,6 @@ def tile_quantuminspiredneuralcore_pb_k_kernel(
                     load_e(first_step, steps)
             if t < len(PIECES):
                 w_raw_of[t] = load_w(t)
-            if t == len(PIECES):
-                path_raw_of[0] = load_weight_rows(path_w.rearrange("w (p t) n -> p w t n", t=PACK))
 
         for t in range(3):
             load_for_round(t)
@@ -325,6 +321,7 @@ def tile_quantuminspiredneuralcore_pb_k_kernel(
                 multiply(t - 1)
 
         stream_round(0)
+        path_raw = load_weight_rows(path_w.rearrange("w (p t) n -> p w t n", t=PACK))
         load_vectors((ENT_PB, ent_pb))
         h_sb = consts.tile([P, TILES, D], BF16, name="h_sb")
         nc.sync.dma_start(out=h_sb[:], in_=h.rearrange("b s d -> s b d"))
@@ -334,10 +331,13 @@ def tile_quantuminspiredneuralcore_pb_k_kernel(
             nc.tensor.transpose(
                 out=vec_bank[:, s, :], in_=path_rows[:, s * P : (s + 1) * P], identity=ident_bf16[:]
             )
-        for t in range(2, LATE_ROUND):
+        for t in range(2, PATH_ROUND):
             stream_round(t)
+        path_grp = regroup_weights(path_raw)
+        stream_round(PATH_ROUND)
+        path_op = quantise_weights(path_grp, 0, 2, consts, "_path")
         load_vectors((LN3_G, ln3_g), (LN3_B, ln3_b), (LN4_G, ln4_g), (LN4_B, ln4_b))
-        for t in range(LATE_ROUND, STEPS):
+        for t in range(PATH_ROUND + 1, STEPS):
             stream_round(t)
         h_bias_bank = [spread_row(ENT_PB, banks, "h_bias_bank%d" % i, plus=h_sb[:, i, :]) for i in range(TILES)]
         ln4_g_bank = spread_row(LN4_G, row_banks, "ln4_g_bank")
@@ -348,10 +348,6 @@ def tile_quantuminspiredneuralcore_pb_k_kernel(
         for t in range(STEPS + 1, len(PIECES) + 1):
             stream_round(t)
         h_bias = [to_sbuf(h_bias_bank[i], "h_bias%d" % i) for i in range(TILES)]
-        path_raw = path_raw_of[0]
-        path_grp = grouped_tile(path_raw)
-        regroup_on_vector(path_raw, path_grp, V_PATH_COLS)
-        regroup_on_scalar(path_raw, path_grp, 0, V_PATH_COLS)
         nc.scalar.activation(out=table_warm[:], in_=eps[:], func=ACT.Abs_reciprocal_sqrt)
 
         def inverse_std(x, x_sum, label):
@@ -425,10 +421,10 @@ def tile_quantuminspiredneuralcore_pb_k_kernel(
             hn_codes, hn_scales = hn_op
             products = []
             for w in range(2):
-                path_codes, path_scales = path_op[w]
+                path_codes, path_scales = path_op
                 product = banks.tile([P, SLICES, P], F32, name="product", tag="bank")
                 for f in range(SLICES):
-                    first = f * P
+                    first = w * D + f * P
                     nc.tensor.matmul_mx(
                         out=product[:, f, :],
                         lhsT=path_codes[:, first : first + P].bitcast(FP8X4),
@@ -473,7 +469,6 @@ def tile_quantuminspiredneuralcore_pb_k_kernel(
         both = range(TILES)
         x = [add_rows(acc[i][:], 1.0, h_bias[i][:], "x%d" % i) for i in both]
         rstd = [inverse_std(x[i][0], x[i][1], "_a%d" % i) for i in both]
-        regroup_on_scalar(path_raw, path_grp, 1, V_PATH_COLS)
         neg_mean = [negative_mean(x[i][1], "_a%d" % i) for i in both]
         centred = [centre(x[i][0], neg_mean[i], ln3_g_bank, "_a%d" % i) for i in both]
         hn_rounded = [scale_and_shift(centred[i], rstd[i], ln3_b_bank, "hn_rounded%d" % i, BF16) for i in both]
@@ -482,11 +477,7 @@ def tile_quantuminspiredneuralcore_pb_k_kernel(
         hn_bank = [transpose_hn(hn_rounded[i]) for i in both]
         keep_clock_up(idle_bank, 1)
         hn_grp = [group_hn(i, hn_bank[i]) for i in both]
-        path_op = []
-        hn_op = []
-        for i in both:
-            path_op.append(quantise_weights(path_grp, i, 1, consts, "_path%d" % i))
-            hn_op.append(quantise_hn(i, hn_grp[i]))
+        hn_op = [quantise_hn(i, hn_grp[i]) for i in both]
         products = [pathways(hn_op[i]) for i in both]
         interf = [interfere(i, products[i]) for i in both]
         interf_bank = [transpose_back(i, interf[i]) for i in both]

import math
from contextlib import ExitStack

import concourse.masks as masks
import concourse.mybir as mybir

F32 = mybir.dt.float32
BF16 = mybir.dt.bfloat16
U32 = mybir.dt.uint32
U8 = mybir.dt.uint8
FP8X4 = mybir.dt.float8_e4m3fn_x4
ALU = mybir.AluOpType
ACT = mybir.ActivationFunctionType

P = 128
PACK = 4
K_PASS = P * PACK
TILES = 2
D = 512
K = 16384
SLICES = D // P
EPS = 1e-5

STEP_PASSES = 2
STEPS = K // (STEP_PASSES * K_PASS)
PIECES = (
    [(c, 1) for c in range(STEP_PASSES)]
    + [(s * STEP_PASSES, STEP_PASSES) for s in range(1, STEPS - 1)]
    + [(K // K_PASS - STEP_PASSES + c, 1) for c in range(STEP_PASSES)]
)
AHEAD = 5
E_LOADS = [(0, 1), (1, 1)] + [(s, 2) for s in range(2, STEPS, 2)]
SMALL_ROUND = 3
PATH_ROUND = 6

V_COLS = 288

FLOPS = 2 * TILES * P * K * D + 2 * 2 * TILES * P * D * D

PATH_B, LN3_B_COLUMN, PHASE = 0, 2, 3
MOD = 3
SHIFT = 5
COLUMNS = 6
ENT_PB, LN3_G, LN3_B, LN4_G, LN4_B = range(5)

TWO_PI_HI = 6.28125
TWO_PI_MID = 0.0019353071693331003
TWO_PI_LO = 1.0253131677018246e-11
INV_TWO_PI = 0.15915493667125702
QUARTER_PI = math.pi / 4
SQRT_2 = math.sqrt(2.0)
PI_BELOW = 3.141592502593994
ROUND_MAGIC = 12582912.0


def tile_quantuminspiredneuralcore_pb_k_kernel(
    tc, e, h, ent_pw, ent_pb, ln3_g, ln3_b, path_w, path_b, phase, ln4_g, ln4_b, out
):
    nc = tc.nc
    with ExitStack() as ctx:
        consts = ctx.enter_context(tc.tile_pool(name="consts", bufs=1))
        e_raws = ctx.enter_context(tc.tile_pool(name="e_raws", bufs=AHEAD))
        w_raws = ctx.enter_context(tc.tile_pool(name="w_raws", bufs=AHEAD + 2))
        grouped = ctx.enter_context(tc.tile_pool(name="grouped", bufs=3))
        w_quant = ctx.enter_context(tc.tile_pool(name="w_quant", bufs=3))
        e_quant = ctx.enter_context(tc.tile_pool(name="e_quant", bufs=4))
        work = ctx.enter_context(tc.tile_pool(name="work", bufs=1))
        small = ctx.enter_context(tc.tile_pool(name="small", bufs=1))
        accs = ctx.enter_context(tc.psum_pool(name="accs", bufs=1))
        banks = ctx.enter_context(tc.psum_pool(name="banks", bufs=4))
        row_banks = ctx.enter_context(tc.psum_pool(name="row_banks", bufs=2))

        def load_weight_rows(view):
            w_raw = w_raws.tile(list(view.shape), BF16, name="w_raw", tag="w_raw")
            nc.sync.dma_start(out=w_raw[:], in_=view)
            return w_raw

        def load_w(piece):
            first_pass, passes = PIECES[piece]
            rows = ent_pw[first_pass * K_PASS : (first_pass + passes) * K_PASS, :]
            return load_weight_rows(rows.rearrange("(c p t) n -> p c t n", p=P, t=PACK))

        e_raw_of = {}

        def load_e(first_step, steps):
            width = STEP_PASSES * K_PASS
            e_raw = e_raws.tile([P, TILES, steps * width], BF16, name="e_raw", tag="e_raw")
            nc.sync.dma_start(
                out=e_raw[:],
                in_=e[:, :, first_step * width : (first_step + steps) * width].rearrange("b s k -> s b k"),
            )
            for s in range(steps):
                e_raw_of[first_step + s] = (e_raw, s)

        def grouped_tile(w_raw):
            return grouped.tile([P, w_raw.shape[1], D, PACK], BF16, name="w_grp", tag="w_grp", align_bytes=64)

        def regroup_on_vector(w_raw, w_grp, columns):
            nc.vector.tensor_copy(
                out=w_grp[:, :, 0:columns, :].rearrange("p c (a i) t -> p c a t i", i=4),
                in_=w_raw[:, :, :, 0:columns].rearrange("p c t (a i) -> p c a t i", i=4),
            )

        def regroup_on_scalar(w_raw, w_grp, c, columns):
            nc.scalar.copy(
                out=w_grp[:, c, columns:D, :].rearrange("p (a i) t -> p a t i", i=4),
                in_=w_raw[:, c, :, columns:D].rearrange("p t (a i) -> p a t i", i=4),
            )

        def regroup_weights(w_raw):
            w_grp = grouped_tile(w_raw)
            regroup_on_vector(w_raw, w_grp, V_COLS)
            for c in range(w_raw.shape[1]):
                regroup_on_scalar(w_raw, w_grp, c, V_COLS)
            return w_grp

        def quantise_weights(w_grp, first, passes, pool, label=""):
            name = "w_codes" + label
            codes = pool.tile([P, passes * D], U32, name=name, tag=name, align_bytes=64)
            name = "w_scales" + label
            scales = pool.tile([P, passes * D], U8, name=name, tag=name, align_bytes=64)
            nc.vector.quantize_mx(
                out=codes[:].bitcast(FP8X4),
                scales=scales[:],
                in_=w_grp[:, first : first + passes].rearrange("p c n t -> p (c n t)"),
            )
            return codes, scales

        def transpose_e(e_raw, step):
            words = K_PASS // 2
            planes = []
            for i in range(TILES):
                e_words = e_raw[:, i, :].bitcast(F32)
                bank = banks.tile([P, STEP_PASSES, 2, P], F32, name="e_bank", tag="bank")
                for c in range(STEP_PASSES):
                    first = (step * STEP_PASSES + c) * words
                    for u in range(2):
                        nc.tensor.transpose(
                            out=bank[:, c, u, :],
                            in_=e_words[:, first + u : first + words : 2],
                            identity=ident_f32[:],
                        )
                planes.append(bank)
            return planes

        def copy_e(planes):
            e_grp = grouped.tile(
                [P, TILES * STEP_PASSES * P * 2], F32, name="e_grp", tag="e_grp", align_bytes=64
            )
            per_tile = STEP_PASSES * P * 2
            for i in range(TILES):
                nc.scalar.copy(
                    out=e_grp[:, i * per_tile : (i + 1) * per_tile].rearrange(
                        "p (c r u) -> p c r u", c=STEP_PASSES, u=2
                    ),
                    in_=planes[i][:].rearrange("p c u r -> p c r u"),
                )
            return e_grp

        def quantise_e(e_grp):
            codes = e_quant.tile([P, TILES * STEP_PASSES * P], U32, name="e_codes", tag="e_codes", align_bytes=64)
            scales = e_quant.tile([P, TILES * STEP_PASSES * P], U8, name="e_scales", tag="e_scales", align_bytes=64)
            nc.vector.quantize_mx(
                out=codes[:].bitcast(FP8X4), scales=scales[:], in_=e_grp[:].bitcast(BF16)
            )
            return codes, scales

        def multiply(piece):
            first_pass, passes = PIECES[piece]
            e_codes, e_scales = e_op[first_pass // STEP_PASSES]
            w_codes, w_scales = w_op[piece]
            for c in range(passes):
                k_pass = first_pass + c
                w_cols = slice(c * D, (c + 1) * D)
                for i in range(TILES):
                    e_first = (i * STEP_PASSES + k_pass % STEP_PASSES) * P
                    e_cols = slice(e_first, e_first + P)
                    nc.tensor.matmul_mx(
                        out=acc[i][:],
                        lhsT=e_codes[:, e_cols].bitcast(FP8X4),
                        lhsT_scale=e_scales[:, e_cols],
                        rhs=w_codes[:, w_cols].bitcast(FP8X4),
                        rhs_scale=w_scales[:, w_cols],
                        start=(k_pass == 0),
                        stop=(k_pass == K // K_PASS - 1),
                    )

        ctx.enter_context(tc.manual_schedule())

        path_rows = consts.tile([P, D], BF16, name="path_rows")
        nc.vector.memset(path_rows[:].bitcast(mybir.dt.int32), 0)
        eps = consts.tile([P, 1], F32, name="eps")
        nc.vector.memset(eps[:], EPS)
        vec_rows = consts.tile([P, D], BF16, name="vec_rows")

        def as_row(vector):
            return vector.rearrange("(o d) -> o d", o=1)

        w_raw_of = {}

        def load_vectors(*rows):
            for row, vector in rows:
                nc.sync.dma_start(out=vec_rows[row : row + 1, :], in_=as_row(vector))

        def load_for_round(t):
            for first_step, steps in E_LOADS:
                if first_step == t - 1:
                    load_e(first_step, steps)
            if t < len(PIECES):
                w_raw_of[t] = load_w(t)

        for t in range(3):
            load_for_round(t)
        for row, vector in ((PHASE, phase), (PATH_B, path_b), (LN3_B_COLUMN, as_row(ln3_b))):
            nc.sync.dma_start(out=path_rows[row : row + vector.shape[0], :], in_=vector)
        for t in range(3, AHEAD):
            load_for_round(t)

        ident_bf16 = consts.tile([P, P], BF16, name="ident_bf16")
        masks.make_identity(nc, ident_bf16[:])
        ident_f32 = consts.tile([P, P], F32, name="ident_f32")
        masks.make_identity(nc, ident_f32[:])
        nc.gpsimd.memset(vec_rows[:], 0.0)
        table_warm = consts.tile([P, 1], F32, name="table_warm")
        nc.scalar.activation(out=table_warm[:], in_=eps[:], func=ACT.Sin)

        def spread_row(row, pool, name, plus=None):
            bank = pool.tile([P, D], F32, name=name, tag="bank")
            if plus is not None:
                nc.tensor.matmul(out=bank[:], lhsT=ident_bf16[:], rhs=plus, start=True, stop=False)
            nc.tensor.matmul(
                out=bank[:],
                lhsT=ident_bf16[:, row : row + 1].to_broadcast([P, P]),
                rhs=vec_rows[:],
                start=plus is None,
                stop=True,
            )
            return bank

        def to_sbuf(bank, name):
            row = consts.tile([P, D], F32, name=name)
            nc.scalar.copy(out=row[:], in_=bank[:])
            return row

        acc = [accs.tile([P, D], F32, name="acc%d" % i, tag="acc%d" % i) for i in range(TILES)]

        def planes_of(step):
            return transpose_e(*e_raw_of[step])

        cols = consts.tile([P, SLICES, COLUMNS], F32, name="cols")
        phases = consts.tile([P, SLICES, 2], F32, name="phases")
        turns = consts.tile([P, SLICES, 2], F32, name="turns")
        angle = consts.tile([P, SLICES, 2], F32, name="angle")
        sine = consts.tile([P, SLICES, 2], F32, name="sine")
        weighted_b = consts.tile([P, SLICES, 2], F32, name="weighted_b")
        mods = cols[:, :, MOD : MOD + 2]
        shift = cols[:, :, SHIFT : SHIFT + 1]

        def add_turns(of_a_turn, to):
            nc.vector.scalar_tensor_tensor(
                out=angle[:], in0=turns[:], scalar=-of_a_turn, in1=to, op0=ALU.mult, op1=ALU.add
            )

        def scalars(out, in0, scalar1, op0, scalar2=None, op1=None):
            if op1 is None:
                nc.vector.tensor_scalar(out=out, in0=in0, scalar1=scalar1, scalar2=None, op0=op0)
            else:
                nc.vector.tensor_scalar(out=out, in0=in0, scalar1=scalar1, scalar2=scalar2, op0=op0, op1=op1)

        small_steps = [
            lambda: nc.vector.tensor_copy(out=cols[:, :, 0:MOD], in_=vec_bank[:, :, 0:MOD]),
            lambda: scalars(phases[:], vec_bank[:, :, PHASE : PHASE + 2], QUARTER_PI, ALU.add),
            lambda: scalars(turns[:], phases[:], INV_TWO_PI, ALU.mult, ROUND_MAGIC, ALU.add),
            lambda: scalars(turns[:], turns[:], ROUND_MAGIC, ALU.subtract),
            lambda: add_turns(TWO_PI_HI, phases[:]),
            lambda: add_turns(TWO_PI_MID, angle[:]),
            lambda: add_turns(TWO_PI_LO, angle[:]),
            lambda: scalars(angle[:], angle[:], PI_BELOW, ALU.min, -PI_BELOW, ALU.max),
            lambda: nc.scalar.activation(out=sine[:], in_=angle[:], func=ACT.Sin),
            lambda: scalars(mods, sine[:], SQRT_2, ALU.mult),
            lambda: nc.vector.tensor_tensor(
                out=weighted_b[:], in0=cols[:, :, PATH_B : PATH_B + 2], in1=mods, op=ALU.mult
            ),
            lambda: nc.vector.tensor_tensor(
                out=shift, in0=weighted_b[:, :, 0:1], in1=weighted_b[:, :, 1:2], op=ALU.add
            ),
            lambda: nc.vector.tensor_tensor(
                out=shift, in0=shift, in1=cols[:, :, LN3_B_COLUMN : LN3_B_COLUMN + 1], op=ALU.add
            ),
        ]

        def small_step(t, place):
            step = 3 * (t - SMALL_ROUND) + place
            if 0 <= step < len(small_steps):
                small_steps[step]()

        e_planes = {}
        e_grp_of = {}
        e_op = {}
        w_grp_of = {}
        w_op = {}

        def stream_round(t):
            load_for_round(t + AHEAD)
            if t < STEPS:
                e_planes[t] = transpose_e(*e_raw_of[t])
            if 1 <= t <= STEPS:
                e_grp_of[t - 1] = copy_e(e_planes[t - 1])
            if 2 <= t <= STEPS + 1:
                e_op[t - 2] = quantise_e(e_grp_of[t - 2])
            small_step(t, 0)
            if t >= 1:
                w_op[t - 1] = quantise_weights(w_grp_of[t - 1], 0, PIECES[t - 1][1], w_quant)
            small_step(t, 1)
            if t < len(PIECES):
                w_grp_of[t] = regroup_weights(w_raw_of[t])
            small_step(t, 2)
            if t == 2:
                multiply(0)
            if t >= 2:
                multiply(t - 1)

        stream_round(0)
        path_raw = load_weight_rows(path_w.rearrange("w (p t) n -> p w t n", t=PACK))
        load_vectors((ENT_PB, ent_pb))
        h_sb = consts.tile([P, TILES, D], BF16, name="h_sb")
        nc.sync.dma_start(out=h_sb[:], in_=h.rearrange("b s d -> s b d"))
        stream_round(1)
        vec_bank = row_banks.tile([P, SLICES, P], BF16, name="vec_bank", tag="bank")
        for s in range(SLICES):
            nc.tensor.transpose(
                out=vec_bank[:, s, :], in_=path_rows[:, s * P : (s + 1) * P], identity=ident_bf16[:]
            )
        for t in range(2, PATH_ROUND):
            stream_round(t)
        path_grp = regroup_weights(path_raw)
        stream_round(PATH_ROUND)
        path_op = quantise_weights(path_grp, 0, 2, consts, "_path")
        load_vectors((LN3_G, ln3_g), (LN3_B, ln3_b), (LN4_G, ln4_g), (LN4_B, ln4_b))
        for t in range(PATH_ROUND + 1, STEPS):
            stream_round(t)
        h_bias_bank = [spread_row(ENT_PB, banks, "h_bias_bank%d" % i, plus=h_sb[:, i, :]) for i in range(TILES)]
        ln4_g_bank = spread_row(LN4_G, row_banks, "ln4_g_bank")
        ln4_b_bank = spread_row(LN4_B, row_banks, "ln4_b_bank")
        stream_round(STEPS)
        ln3_g_bank = spread_row(LN3_G, banks, "ln3_g_bank")
        ln3_b_bank = spread_row(LN3_B, banks, "ln3_b_bank")
        for t in range(STEPS + 1, len(PIECES) + 1):
            stream_round(t)
        h_bias = [to_sbuf(h_bias_bank[i], "h_bias%d" % i) for i in range(TILES)]
        nc.scalar.activation(out=table_warm[:], in_=eps[:], func=ACT.Abs_reciprocal_sqrt)

        def inverse_std(x, x_sum, label):
            squares = work.tile([P, D], F32, name="squares" + label)
            sum_sq = small.tile([P, 1], F32, name="sum_sq" + label)
            nc.scalar.activation(
                out=squares[:], in_=x[:], func=ACT.Square, scale=-float(D), bias=x_sum[:, 0:1], accum_out=sum_sq[:]
            )
            rstd = small.tile([P, 1], F32, name="rstd" + label)
            nc.scalar.activation(
                out=rstd[:], in_=sum_sq[:], func=ACT.Abs_reciprocal_sqrt, bias=eps[:, 0:1], scale=1.0 / D**3
            )
            return rstd

        def negative_mean(x_sum, label):
            neg_mean = small.tile([P, 1], F32, name="neg_mean" + label)
            nc.vector.tensor_scalar(
                out=neg_mean[:], in0=x_sum[:], scalar1=-1.0 / D, scalar2=None, op0=ALU.mult
            )
            return neg_mean

        def centre(x, neg_mean, gain_row, label):
            centred = work.tile([P, D], F32, name="centred" + label)
            nc.vector.scalar_tensor_tensor(
                out=centred[:], in0=x[:], scalar=neg_mean[:, 0:1], in1=gain_row[:], op0=ALU.add, op1=ALU.mult
            )
            return centred

        def scale_and_shift(centred, rstd, shift, name, dtype=F32):
            result = work.tile([P, D], dtype, name=name)
            nc.vector.scalar_tensor_tensor(
                out=result[:], in0=centred[:], scalar=rstd[:, 0:1], in1=shift[:], op0=ALU.mult, op1=ALU.add
            )
            return result

        def add_rows(in0, scale, in1, name):
            total = work.tile([P, D], F32, name=name)
            total_sum = small.tile([P, 1], F32, name=name + "_sum")
            nc.vector.scalar_tensor_tensor(
                out=total[:], in0=in0, scalar=scale, in1=in1, op0=ALU.mult, op1=ALU.add, accum_out=total_sum[:]
            )
            return total, total_sum

        def keep_clock_up(bank, count):
            for n in range(count):
                nc.tensor.matmul(out=bank[:], lhsT=ident_bf16[:], rhs=vec_rows[:], start=True, stop=True)

        def transpose_hn(hn_rounded):
            words = hn_rounded[:].bitcast(F32)
            hn_bank = banks.tile([P, 2, P], F32, name="hn_bank", tag="bank")
            for u in range(2):
                nc.tensor.transpose(
                    out=hn_bank[:, u, :], in_=words[:, u : D // 2 : 2], identity=ident_f32[:]
                )
            return hn_bank

        def group_hn(i, hn_bank):
            hn_grp = work.tile([P, P * 2], F32, name="hn_grp%d" % i, align_bytes=64)
            nc.scalar.copy(
                out=hn_grp[:].rearrange("p (r u) -> p r u", u=2), in_=hn_bank[:].rearrange("p u r -> p r u")
            )
            return hn_grp

        def quantise_hn(i, hn_grp):
            codes = work.tile([P, P], U32, name="hn_codes%d" % i, align_bytes=64)
            scales = work.tile([P, P], U8, name="hn_scales%d" % i, align_bytes=64)
            nc.vector.quantize_mx(out=codes[:].bitcast(FP8X4), scales=scales[:], in_=hn_grp[:].bitcast(BF16))
            return codes, scales

        def pathways(hn_op):
            hn_codes, hn_scales = hn_op
            products = []
            for w in range(2):
                path_codes, path_scales = path_op
                product = banks.tile([P, SLICES, P], F32, name="product", tag="bank")
                for f in range(SLICES):
                    first = w * D + f * P
                    nc.tensor.matmul_mx(
                        out=product[:, f, :],
                        lhsT=path_codes[:, first : first + P].bitcast(FP8X4),
                        lhsT_scale=path_scales[:, first : first + P],
                        rhs=hn_codes[:].bitcast(FP8X4),
                        rhs_scale=hn_scales[:],
                        start=True,
                        stop=True,
                    )
                products.append(product)
            return products

        def interfere(i, products):
            first_term = work.tile([P, SLICES, P], F32, name="first_term%d" % i)
            interf = work.tile([P, SLICES, P], F32, name="interf%d" % i)
            for f in range(SLICES):
                nc.scalar.activation(
                    out=first_term[:, f, :],
                    in_=products[0][:, f, :],
                    func=ACT.Identity,
                    scale=cols[:, f, MOD : MOD + 1],
                    bias=cols[:, f, SHIFT : SHIFT + 1],
                )
                nc.vector.scalar_tensor_tensor(
                    out=interf[:, f, :],
                    in0=products[1][:, f, :],
                    scalar=cols[:, f, MOD + 1 : MOD + 2],
                    in1=first_term[:, f, :],
                    op0=ALU.mult,
                    op1=ALU.add,
                )
            return interf

        def transpose_back(i, interf):
            bank = accs.tile([P, D], F32, name="interf_bank%d" % i, tag="acc%d" % i)
            for f in range(SLICES):
                nc.tensor.transpose(
                    out=bank[:, f * P : (f + 1) * P], in_=interf[:, f, :], identity=ident_f32[:]
                )
            return bank

        both = range(TILES)
        x = [add_rows(acc[i][:], 1.0, h_bias[i][:], "x%d" % i) for i in both]
        rstd = [inverse_std(x[i][0], x[i][1], "_a%d" % i) for i in both]
        neg_mean = [negative_mean(x[i][1], "_a%d" % i) for i in both]
        centred = [centre(x[i][0], neg_mean[i], ln3_g_bank, "_a%d" % i) for i in both]
        hn_rounded = [scale_and_shift(centred[i], rstd[i], ln3_b_bank, "hn_rounded%d" % i, BF16) for i in both]
        idle_bank = accs.tile([P, D], F32, name="idle_bank", tag="acc1")
        keep_clock_up(idle_bank, 7)
        hn_bank = [transpose_hn(hn_rounded[i]) for i in both]
        keep_clock_up(idle_bank, 1)
        hn_grp = [group_hn(i, hn_bank[i]) for i in both]
        hn_op = [quantise_hn(i, hn_grp[i]) for i in both]
        products = [pathways(hn_op[i]) for i in both]
        interf = [interfere(i, products[i]) for i in both]
        interf_bank = [transpose_back(i, interf[i]) for i in both]
        y = [add_rows(centred[i][:], rstd[i][:, 0:1], interf_bank[i][:], "y%d" % i) for i in both]
        rstd = [inverse_std(y[i][0], y[i][1], "_b%d" % i) for i in both]
        neg_mean = [negative_mean(y[i][1], "_b%d" % i) for i in both]
        centred = [centre(y[i][0], neg_mean[i], ln4_g_bank, "_b%d" % i) for i in both]
        for i in both:
            result = work.tile([P, D], F32, name="result%d" % i)
            width = D if i < TILES - 1 else D // 2
            for first in range(0, D, width):
                part = slice(first, first + width)
                nc.vector.scalar_tensor_tensor(
                    out=result[:, part],
                    in0=centred[i][:, part],
                    scalar=rstd[i][:, 0:1],
                    in1=ln4_b_bank[:, part],
                    op0=ALU.mult,
                    op1=ALU.add,
                )
                nc.sync.dma_start(out=out[i, :, part], in_=result[:, part])
